import numpy as np
import ml_dtypes


def mxq(x, axis, fmt="e4m3"):
    dtype, down = {"e4m3": (ml_dtypes.float8_e4m3fn, 7), "e5m2": (ml_dtypes.float8_e5m2, 14)}[fmt]
    v = np.moveaxis(np.asarray(x, np.float32).astype(ml_dtypes.bfloat16).astype(np.float64), axis, -1)
    blocks = v.reshape(v.shape[:-1] + (-1, 32))
    amax = np.abs(blocks).max(-1, keepdims=True)
    byte = np.maximum(np.where(amax > 0, np.frexp(amax)[1] - 1 + 127, 0) - down, 1)
    scale = np.exp2(byte - 127.0)
    codes = (blocks / scale).astype(np.float32).astype(dtype).astype(np.float64)
    return np.moveaxis((codes * scale).reshape(v.shape), -1, axis)


WIDE = False


def mx_kscale(k):
    if not WIDE:
        return np.ones(k)
    levels = np.array([10, -10, 5, -5, 0])
    if k % 512:
        return np.exp2(np.random.permutation(np.resize(levels, k // 32))).repeat(32)
    a = np.empty((k // 512, 16))
    for p in range(k // 512):
        a[p, :8] = np.random.permutation(np.resize(levels, 8))
        for g in range(8):
            far = levels[np.abs(levels - a[p, g]) >= 10]
            a[p, g + 8] = far[np.random.randint(len(far))]
    return np.exp2(a.ravel()).repeat(32)


BF16 = ml_dtypes.bfloat16


def bf(x):
    return np.asarray(x, np.float32).astype(BF16)


def f64(x):
    return np.asarray(x).astype(np.float64)


SEQ, B, HID, NH, HD, RD = 128, 4, 2048, 16, 128, 32
W = NH * HD
BASE = 10000.0


def rope_tables():
    inv_freq = 1.0 / BASE ** (f64(np.arange(0, RD, 2)) / RD)
    fr = f64(np.arange(SEQ))[:, None] * inv_freq[None, :]
    ang = np.concatenate([fr, fr], axis=-1)
    return np.cos(ang), np.sin(ang)


def apply_rotary(t, cos, sin):
    rot = t[..., : 2 * RD].reshape(SEQ, B, NH, RD, 2)
    c = cos[:, None, None, :]
    s = sin[:, None, None, :]
    re = rot[..., 0] * c - rot[..., 1] * s
    im = rot[..., 0] * s + rot[..., 1] * c
    rot2 = np.stack([re, im], axis=-1).reshape(SEQ, B, NH, 2 * RD)
    return np.concatenate([rot2, t[..., 2 * RD:]], axis=-1)


def draw0():
    s = mx_kscale(HID)
    sc = 1.0 / np.sqrt(HID)
    return {"x": bf(np.random.standard_normal((SEQ, B, HID)) * s),
            "wq": bf(np.random.standard_normal((W, HID)) * sc / s[None, :]),
            "bq": bf(np.random.standard_normal(W) * 0.3),
            "wk": bf(np.random.standard_normal((W, HID)) * sc / s[None, :]),
            "bk": bf(np.random.standard_normal(W) * 0.3)}


def core(x, wq, bq, wk, bk):
    xq = mxq(f64(x), 2, "e4m3")
    q = ((xq @ mxq(f64(wq), 1, "e4m3").T) + f64(bq)).reshape(SEQ, B, NH, HD)
    k = ((xq @ mxq(f64(wk), 1, "e4m3").T) + f64(bk)).reshape(SEQ, B, NH, HD)
    cos, sin = rope_tables()
    q = apply_rotary(q, cos, sin)
    k = apply_rotary(k, cos, sin)
    return q.transpose(1, 2, 0, 3), k.transpose(1, 2, 0, 3)


def e4m3fn_bytes(y):
    return np.clip(np.asarray(y, np.float64), -448.0, 448.0).astype(np.float32).astype(ml_dtypes.float8_e4m3fn).view(np.uint8)


def e4m3fn_values(b):
    return np.asarray(b, np.uint8).view(ml_dtypes.float8_e4m3fn).astype(np.float64)


def setup_inputs():
    d = draw0()
    x0 = np.asarray(d['wq']).astype(np.float64)
    s = (np.max(np.abs(x0), axis=(0,), keepdims=True) / 448.0).astype(np.float32)
    out = {}
    for k, v in d.items():
        if k == 'wq':
            out['wq_bytes'] = e4m3fn_bytes(x0 / s.astype(np.float64))
            out['wq_scale'] = s
        else:
            out[k] = v
    return out


def reference(x, wq_bytes, wq_scale, bq, wk, bk):
    return core(x, e4m3fn_values(wq_bytes) * wq_scale.astype(np.float64), bq, wk, bk)

@@ -1,0 +1,269 @@
+from contextlib import ExitStack
+import math
+
+import concourse.masks as masks
+import concourse.mybir as mybir
+
+F32 = mybir.dt.float32
+BF16 = mybir.dt.bfloat16
+U32 = mybir.dt.uint32
+U8 = mybir.dt.uint8
+I32 = mybir.dt.int32
+FP8 = mybir.dt.float8_e4m3fn
+FP8X4 = mybir.dt.float8_e4m3fn_x4
+ALU = mybir.AluOpType
+ACT = mybir.ActivationFunctionType
+
+SEQ, B, HID, NH, HD, RD = 128, 4, 2048, 16, 128, 32
+P = 128
+PASSES = HID // 512
+TOK = SEQ * B
+ROT = 2 * RD
+FLOPS = 2 * SEQ * B * HID * 2 * NH * HD
+
+
+def tile_gptneoxattention_pa_kernel(tc, x, wq_bytes, wq_scale, bq, wk, bk, out_0, out_1):
+    nc = tc.nc
+    with ExitStack() as ctx:
+        ctx.enter_context(tc.manual_schedule())
+        const = ctx.enter_context(tc.tile_pool(name="const", bufs=1))
+        rows = ctx.enter_context(tc.tile_pool(name="rows", bufs=16))
+        qbytes = ctx.enter_context(tc.tile_pool(name="qbytes", bufs=16))
+        wide = ctx.enter_context(tc.tile_pool(name="wide", bufs=3))
+        grouped = ctx.enter_context(tc.tile_pool(name="grouped", bufs=4))
+        quant = ctx.enter_context(tc.tile_pool(name="quant", bufs=4))
+        chan = ctx.enter_context(tc.tile_pool(name="chan", bufs=4))
+        outp = ctx.enter_context(tc.tile_pool(name="outp", bufs=4))
+        tmp = ctx.enter_context(tc.tile_pool(name="tmp", bufs=2))
+        tps = ctx.enter_context(tc.psum_pool(name="tps", bufs=4))
+        accs = ctx.enter_context(tc.psum_pool(name="accs", bufs=2))
+        bts = ctx.enter_context(tc.psum_pool(name="bts", bufs=2))
+
+        seq = []
+        for h in range(NH):
+            seq.append((0, h))
+            seq.append((1, h))
+        n_heads = len(seq)
+
+        warm = const.tile([P, 8], F32)
+        nc.vector.memset(warm[:], 0.0)
+        nc.scalar.activation(out=warm[:], in_=warm[:], func=ACT.Sin)
+        ident = const.tile([P, P], F32)
+        masks.make_identity(nc, ident[:])
+        bias_rows = const.tile([P, P], BF16)
+        nc.vector.memset(bias_rows[:], 0.0)
+
+        scale_bc = const.tile([P, HID], F32)
+        scale_row = wq_scale.rearrange("o k -> (o k)")
+        raw = {}
+
+        def load_scale(c):
+            nc.sync.dma_start(out=scale_bc[:, c * 512:(c + 1) * 512], in_=scale_row[c * 512:(c + 1) * 512].partition_broadcast(P))
+
+        def load_head(i):
+            kind, h = seq[i]
+            if kind == 0:
+                wq_bytes_sb = qbytes.tile([P, HID], U8, name="wq_bytes_sb")
+                nc.sync.dma_start(out=wq_bytes_sb[:], in_=wq_bytes[h * P:(h + 1) * P, :])
+                raw[i] = wq_bytes_sb
+            else:
+                row_sb = rows.tile([P, HID], BF16, name="row_sb")
+                nc.sync.dma_start(out=row_sb[:], in_=wk[h * P:(h + 1) * P, :])
+                raw[i] = row_sb
+
+        x_raw = []
+
+        def load_x(b):
+            row_sb = rows.tile([P, HID], BF16, name="row_sb")
+            nc.sync.dma_start(out=row_sb[:], in_=x[:, b, :])
+            x_raw.append(row_sb)
+
+        nc.sync.dma_start(out=bias_rows[0:NH, :], in_=bq.rearrange("(h d) -> h d", d=HD))
+        nc.sync.dma_start(out=bias_rows[NH:2 * NH, :], in_=bk.rearrange("(h d) -> h d", d=HD))
+        load_scale(0)
+        load_head(0)
+        load_scale(1)
+        load_scale(2)
+        load_scale(3)
+        load_head(2)
+        for b in range(B):
+            load_x(b)
+        load_head(1)
+        for i in range(3, n_heads):
+            load_head(i)
+
+        pos = const.tile([P, ROT], F32)
+        nc.gpsimd.iota(out=pos[:], pattern=[[0, ROT]], base=0, channel_multiplier=1, allow_small_or_imprecise_dtypes=True)
+        sign = const.tile([P, ROT], F32)
+        nc.gpsimd.iota(out=sign[:], pattern=[[0, RD], [-2, 2]], base=1, channel_multiplier=0, allow_small_or_imprecise_dtypes=True)
+        ang = const.tile([P, ROT], F32)
+        ang_v = ang[:].rearrange("p (a f e) -> p a f e", a=2, e=2)
+        pos_v = pos[:].rearrange("p (a f e) -> p a f e", a=2, e=2)
+        for f in range(RD // 2):
+            nc.vector.tensor_scalar_mul(out=ang_v[:, :, f, :], in0=pos_v[:, :, f, :], scalar1=1.0 / 10000.0 ** (2.0 * f / RD))
+        arg = const.tile([P, 2 * ROT], F32)
+        nc.vector.tensor_scalar_add(out=arg[:, 0:ROT], in0=ang[:], scalar1=math.pi / 2.0)
+        nc.vector.tensor_tensor(out=arg[:, ROT:2 * ROT], in0=ang[:], in1=sign[:], op=ALU.mult)
+        turns = const.tile([P, 2 * ROT], F32)
+        nc.vector.tensor_scalar_mul(out=turns[:], in0=arg[:], scalar1=1.0 / (2.0 * math.pi))
+        turns_i = const.tile([P, 2 * ROT], I32)
+        nc.vector.tensor_copy(out=turns_i[:], in_=turns[:])
+        turns_f = const.tile([P, 2 * ROT], F32)
+        nc.vector.tensor_copy(out=turns_f[:], in_=turns_i[:])
+        two_pi_hi = 6.28125
+        two_pi_lo = 2.0 * math.pi - two_pi_hi
+        red1 = const.tile([P, 2 * ROT], F32)
+        nc.vector.scalar_tensor_tensor(out=red1[:], in0=turns_f[:], scalar=-two_pi_hi, in1=arg[:], op0=ALU.mult, op1=ALU.add)
+        red2 = const.tile([P, 2 * ROT], F32)
+        nc.vector.scalar_tensor_tensor(out=red2[:], in0=turns_f[:], scalar=-two_pi_lo, in1=red1[:], op0=ALU.mult, op1=ALU.add)
+        over = const.tile([P, 2 * ROT], F32)
+        nc.vector.tensor_single_scalar(out=over[:], in_=red2[:], scalar=math.pi, op=ALU.is_gt)
+        red3 = const.tile([P, 2 * ROT], F32)
+        nc.vector.scalar_tensor_tensor(out=red3[:], in0=over[:], scalar=-2.0 * math.pi, in1=red2[:], op0=ALU.mult, op1=ALU.add)
+        under = const.tile([P, 2 * ROT], F32)
+        nc.vector.tensor_single_scalar(out=under[:], in_=red3[:], scalar=-math.pi, op=ALU.is_lt)
+        red4 = const.tile([P, 2 * ROT], F32)
+        nc.vector.scalar_tensor_tensor(out=red4[:], in0=under[:], scalar=2.0 * math.pi, in1=red3[:], op0=ALU.mult, op1=ALU.add)
+        table = const.tile([P, 2 * ROT], F32)
+        nc.scalar.activation(out=table[:], in_=red4[:], func=ACT.Sin)
+        cos_t = const.tile([P, B, ROT], F32)
+        sin_t = const.tile([P, B, ROT], F32)
+
+        wide_sb = {}
+        grp_sb = {}
+        code_sb = {}
+        acc_sb = {}
+        chan_sb = {}
+        back_sb = {}
+
+        def widen(i, part, parts):
+            if part == 0:
+                wq_wide = wide.tile([P, HID], BF16, name="wq_wide")
+                wide_sb[i] = wq_wide
+            w = HID // parts
+            cols = slice(part * w, (part + 1) * w)
+            nc.vector.tensor_tensor(out=wide_sb[i][:, cols], in0=raw[i][:, cols].bitcast(FP8), in1=scale_bc[:, cols], op=ALU.mult)
+
+        def turn_rows(src, grp_w, slot):
+            words = src[:].bitcast(F32)
+            for a in range(PASSES // 2):
+                tp = tps.tile([P, 2, 2, P], F32, name="tp")
+                for g2 in range(2):
+                    g = 2 * a + g2
+                    for u in range(2):
+                        nc.tensor.transpose(out=tp[:, g2, u, :], in_=words[:, 256 * g + u:256 * (g + 1):2], identity=ident[:])
+                nc.scalar.copy(out=grp_w[:, 2 * a:2 * a + 2, slot * P:(slot + 1) * P, :], in_=tp[:].rearrange("p g u r -> p g r u"))
+
+        def turn(i):
+            kind, h = seq[i]
+            grp = grouped.tile([P, PASSES * P * 4], BF16, name="grp", align_bytes=64)
+            grp_sb[i] = grp
+            src = wide_sb[i] if kind == 0 else raw[i]
+            turn_rows(src, grp[:].bitcast(F32).rearrange("p (g c u) -> p g c u", g=PASSES, u=2), 0)
+
+        def quantize(i):
+            codes = quant.tile([P, PASSES, P], U32, name="w_codes", align_bytes=64)
+            scl = quant.tile([P, PASSES, P], U8, name="w_scl", align_bytes=64)
+            nc.vector.quantize_mx(
+                out=codes[:].rearrange("p g c -> p (g c)").bitcast(FP8X4),
+                scales=scl[:].rearrange("p g c -> p (g c)"),
+                in_=grp_sb[i][:],
+            )
+            code_sb[i] = (codes, scl)
+
+        def multiply(i):
+            kind, h = seq[i]
+            codes, scl = code_sb[i]
+            acc = accs.tile([P, TOK], F32, name="acc")
+            for g in range(PASSES):
+                nc.tensor.matmul_mx(
+                    out=acc[:],
+                    lhsT=codes[:, g, :].bitcast(FP8X4),
+                    lhsT_scale=scl[:, g, :],
+                    rhs=x_codes[:, g, :].bitcast(FP8X4),
+                    rhs_scale=x_scl[:, g, :],
+                    start=(g == 0),
+                    stop=(g == PASSES - 1),
+                )
+            by_chan = chan.tile([P, TOK], F32, name="by_chan")
+            col = kind * NH + h
+            nc.scalar.activation(out=by_chan[:], in_=acc[:], func=ACT.Identity, bias=bias_col[:, col:col + 1], scale=1.0)
+            chan_sb[i] = by_chan
+
+        def turn_back(i):
+            bt = bts.tile([P, B, HD], F32, name="bt")
+            for b in range(B):
+                nc.tensor.transpose(out=bt[:, b, :], in_=chan_sb[i][:, b * P:(b + 1) * P], identity=ident[:])
+            back_sb[i] = bt
+
+        def finish(pair):
+            res_sb = {}
+            parts = {}
+            for i in pair:
+                res = outp.tile([P, B, HD], F32, name="res")
+                res_sb[i] = res
+                nc.scalar.copy(out=res[:, :, ROT:HD], in_=back_sb[i][:, :, ROT:HD])
+            for i in pair:
+                bt = back_sb[i]
+                part_c = tmp.tile([P, B, ROT], F32, name="part_c")
+                part_s = tmp.tile([P, B, ROT], F32, name="part_s")
+                parts[i] = (part_c, part_s)
+                nc.vector.tensor_tensor(out=part_c[:], in0=bt[:, :, 0:ROT], in1=cos_t[:], op=ALU.mult)
+                nc.vector.tensor_tensor(out=part_s[:], in0=bt[:, :, 0:ROT], in1=sin_t[:], op=ALU.mult)
+            for i in pair:
+                kind, h = seq[i]
+                nc.vector.tensor_tensor(
+                    out=res_sb[i][:, :, 0:ROT].rearrange("p b (j e) -> p b j e", e=2),
+                    in0=parts[i][0][:].rearrange("p b (j e) -> p b j e", e=2),
+                    in1=parts[i][1][:].rearrange("p b (j e) -> p b j e", e=2)[:, :, :, ::-1],
+                    op=ALU.add,
+                )
+                dst = out_0 if kind == 0 else out_1
+                nc.sync.dma_start(out=dst[:, h, :, :].rearrange("b s d -> s b d"), in_=res_sb[i][:])
+
+        bias_f = const.tile([P, P], F32)
+        nc.vector.tensor_copy(out=bias_f[:], in_=bias_rows[:])
+        bias_ps = tps.tile([P, 2, 2, P], F32, name="tp")
+        nc.tensor.transpose(out=bias_ps[:, 0, 0, :], in_=bias_f[:], identity=ident[:])
+        for part in range(4):
+            widen(0, part, 4)
+        bias_col = const.tile([P, 2 * NH], F32)
+        nc.vector.tensor_copy(out=bias_col[:], in_=bias_ps[:, 0, 0, 0:2 * NH])
+        for b in range(B):
+            nc.vector.tensor_copy(out=cos_t[:, b, :], in_=table[:, 0:ROT])
+            nc.vector.tensor_copy(out=sin_t[:, b, :], in_=table[:, ROT:2 * ROT])
+        widen(2, 0, 1)
+        turn(0)
+        xg = const.tile([P, PASSES * TOK * 4], BF16, align_bytes=64)
+        xg_w = xg[:].bitcast(F32).rearrange("p (g c u) -> p g c u", g=PASSES, u=2)
+        x_codes = const.tile([P, PASSES, TOK], U32, align_bytes=64)
+        x_scl = const.tile([P, PASSES, TOK], U8, align_bytes=64)
+        for b in range(B):
+            turn_rows(x_raw[b], xg_w, b)
+            for g in range(PASSES):
+                first = (g * TOK + b * P) * 4
+                nc.vector.quantize_mx(
+                    out=x_codes[:, g, b * P:(b + 1) * P].bitcast(FP8X4),
+                    scales=x_scl[:, g, b * P:(b + 1) * P],
+                    in_=xg[:, first:first + 4 * P],
+                )
+        turn(1)
+        quantize(0)
+        quantize(1)
+
+        n_pairs = n_heads // 2
+        for j in range(n_pairs + 1):
+            if j + 2 < n_pairs:
+                widen(2 * (j + 2), 0, 1)
+            if j + 1 < n_pairs:
+                turn(2 * j + 2)
+                turn(2 * j + 3)
+                quantize(2 * j + 2)
+                quantize(2 * j + 3)
+            if j >= 1:
+                turn_back(2 * j - 2)
+                turn_back(2 * j - 1)
+                finish((2 * j - 2, 2 * j - 1))
+            if j < n_pairs:
+                multiply(2 * j)
+                multiply(2 * j + 1)

@@ -52,13 +52,11 @@ def tile_gptneoxattention_pa_kernel(tc, x, wq_bytes, wq_scale, bq, wk, bk, out_0
         masks.make_identity(nc, ident[:])
         bias_rows = const.tile([P, P], BF16)
         nc.vector.memset(bias_rows[:], 0.0)
+        scale_rows = const.tile([P, P], F32)
+        nc.vector.memset(scale_rows[:], 0.0)
 
         scale_bc = const.tile([P, HID], F32)
-        scale_row = wq_scale.rearrange("o k -> (o k)")
         raw = {}
-
-        def load_scale(c):
-            nc.sync.dma_start(out=scale_bc[:, c * 512:(c + 1) * 512], in_=scale_row[c * 512:(c + 1) * 512].partition_broadcast(P))
 
         def load_head(i):
             kind, h = seq[i]
@@ -78,19 +76,28 @@ def tile_gptneoxattention_pa_kernel(tc, x, wq_bytes, wq_scale, bq, wk, bk, out_0
             nc.sync.dma_start(out=row_sb[:], in_=x[:, b, :])
             x_raw.append(row_sb)
 
+        nc.sync.dma_start(out=scale_rows[0:HID // P, :], in_=wq_scale.rearrange("o (c j) -> (o c) j", j=P))
         nc.sync.dma_start(out=bias_rows[0:NH, :], in_=bq.rearrange("(h d) -> h d", d=HD))
         nc.sync.dma_start(out=bias_rows[NH:2 * NH, :], in_=bk.rearrange("(h d) -> h d", d=HD))
-        load_scale(0)
         load_head(0)
-        load_scale(1)
-        load_scale(2)
-        load_scale(3)
         load_head(2)
         for b in range(B):
             load_x(b)
         load_head(1)
         for i in range(3, n_heads):
             load_head(i)
+
+        sc_ps = tps.tile([P, 2, 2, P], F32, name="tp")
+        nc.tensor.transpose(out=sc_ps[:, 0, 0, :], in_=scale_rows[:], identity=ident[:])
+        scale_col = const.tile([P, HID // P], F32)
+        nc.scalar.copy(out=scale_col[:], in_=sc_ps[:, 0, 0, 0:HID // P])
+        for q in range(4):
+            bc_ps = tps.tile([P, 2, 2, P], F32, name="tp")
+            for a in range(2):
+                for u in range(2):
+                    c = 4 * q + 2 * a + u
+                    nc.tensor.transpose(out=bc_ps[:, a, u, :], in_=scale_col[:, c:c + 1].to_broadcast([P, P]), identity=ident[:])
+            nc.scalar.copy(out=scale_bc[:, q * 512:(q + 1) * 512], in_=bc_ps[:].rearrange("p a u r -> p (a u r)"))
 
         pos = const.tile([P, ROT], F32)
         nc.gpsimd.iota(out=pos[:], pattern=[[0, ROT]], base=0, channel_multiplier=1, allow_small_or_imprecise_dtypes=True)

@@ -30,20 +30,13 @@ def tile_gptneoxattention_pa_kernel(tc, x, wq_bytes, wq_scale, bq, wk, bk, out_0
         rows = ctx.enter_context(tc.tile_pool(name="rows", bufs=16))
         qbytes = ctx.enter_context(tc.tile_pool(name="qbytes", bufs=16))
         wide = ctx.enter_context(tc.tile_pool(name="wide", bufs=3))
-        grouped = ctx.enter_context(tc.tile_pool(name="grouped", bufs=4))
-        quant = ctx.enter_context(tc.tile_pool(name="quant", bufs=4))
-        chan = ctx.enter_context(tc.tile_pool(name="chan", bufs=4))
-        outp = ctx.enter_context(tc.tile_pool(name="outp", bufs=4))
-        tmp = ctx.enter_context(tc.tile_pool(name="tmp", bufs=2))
+        grouped = ctx.enter_context(tc.tile_pool(name="grouped", bufs=2))
+        quant = ctx.enter_context(tc.tile_pool(name="quant", bufs=3))
+        chan = ctx.enter_context(tc.tile_pool(name="chan", bufs=2))
+        outp = ctx.enter_context(tc.tile_pool(name="outp", bufs=3))
         tps = ctx.enter_context(tc.psum_pool(name="tps", bufs=4))
         accs = ctx.enter_context(tc.psum_pool(name="accs", bufs=2))
         bts = ctx.enter_context(tc.psum_pool(name="bts", bufs=2))
-
-        seq = []
-        for h in range(NH):
-            seq.append((0, h))
-            seq.append((1, h))
-        n_heads = len(seq)
 
         warm = const.tile([P, 8], F32)
         nc.vector.memset(warm[:], 0.0)
@@ -56,18 +49,18 @@ def tile_gptneoxattention_pa_kernel(tc, x, wq_bytes, wq_scale, bq, wk, bk, out_0
         nc.vector.memset(scale_rows[:], 0.0)
 
         scale_bc = const.tile([P, HID], F32)
-        raw = {}
+        raw_q = {}
+        raw_k = {}
 
-        def load_head(i):
-            kind, h = seq[i]
-            if kind == 0:
-                wq_bytes_sb = qbytes.tile([P, HID], U8, name="wq_bytes_sb")
-                nc.sync.dma_start(out=wq_bytes_sb[:], in_=wq_bytes[h * P:(h + 1) * P, :])
-                raw[i] = wq_bytes_sb
-            else:
-                row_sb = rows.tile([P, HID], BF16, name="row_sb")
-                nc.sync.dma_start(out=row_sb[:], in_=wk[h * P:(h + 1) * P, :])
-                raw[i] = row_sb
+        def load_q(h):
+            wq_bytes_sb = qbytes.tile([P, HID], U8, name="wq_bytes_sb")
+            nc.sync.dma_start(out=wq_bytes_sb[:], in_=wq_bytes[h * P:(h + 1) * P, :])
+            raw_q[h] = wq_bytes_sb
+
+        def load_k(h):
+            row_sb = rows.tile([P, HID], BF16, name="row_sb")
+            nc.sync.dma_start(out=row_sb[:], in_=wk[h * P:(h + 1) * P, :])
+            raw_k[h] = row_sb
 
         x_raw = []
 
@@ -77,15 +70,19 @@ def tile_gptneoxattention_pa_kernel(tc, x, wq_bytes, wq_scale, bq, wk, bk, out_0
             x_raw.append(row_sb)
 
         nc.sync.dma_start(out=scale_rows[0:HID // P, :], in_=wq_scale.rearrange("o (c j) -> (o c) j", j=P))
-        nc.sync.dma_start(out=bias_rows[0:NH, :], in_=bq.rearrange("(h d) -> h d", d=HD))
-        nc.sync.dma_start(out=bias_rows[NH:2 * NH, :], in_=bk.rearrange("(h d) -> h d", d=HD))
-        load_head(0)
-        load_head(2)
+        for kind, vec in ((0, bq), (1, bk)):
+            halves = vec.rearrange("(h x r) -> x h r", x=2, r=ROT)
+            for half in range(2):
+                nc.sync.dma_start(out=bias_rows[half * NH:(half + 1) * NH, kind * ROT:(kind + 1) * ROT], in_=halves[half])
+        load_q(0)
+        load_q(1)
         for b in range(B):
             load_x(b)
-        load_head(1)
-        for i in range(3, n_heads):
-            load_head(i)
+        load_k(0)
+        load_k(1)
+        for h in range(2, NH):
+            load_q(h)
+            load_k(h)
 
         sc_ps = tps.tile([P, 2, 2, P], F32, name="tp")
         nc.tensor.transpose(out=sc_ps[:, 0, 0, :], in_=scale_rows[:], identity=ident[:])
@@ -131,27 +128,25 @@ def tile_gptneoxattention_pa_kernel(tc, x, wq_bytes, wq_scale, bq, wk, bk, out_0
         nc.vector.tensor_single_scalar(out=under[:], in_=red3[:], scalar=-math.pi, op=ALU.is_lt)
         red4 = const.tile([P, 2 * ROT], F32)
         nc.vector.scalar_tensor_tensor(out=red4[:], in0=under[:], scalar=2.0 * math.pi, in1=red3[:], op0=ALU.mult, op1=ALU.add)
-        table = const.tile([P, 2 * ROT], F32)
-        nc.scalar.activation(out=table[:], in_=red4[:], func=ACT.Sin)
-        cos_t = const.tile([P, B, ROT], F32)
-        sin_t = const.tile([P, B, ROT], F32)
+        table = const.tile([P, 2, 2, ROT], F32)
+        for kind in range(2):
+            nc.scalar.activation(out=table[:, :, kind, :], in_=red4[:].rearrange("p (c r) -> p c r", c=2), func=ACT.Sin)
 
         wide_sb = {}
         grp_sb = {}
         code_sb = {}
-        acc_sb = {}
         chan_sb = {}
         back_sb = {}
 
-        def widen(i, part, parts):
+        def widen(h, part, parts):
             if part == 0:
                 wq_wide = wide.tile([P, HID], BF16, name="wq_wide")
-                wide_sb[i] = wq_wide
+                wide_sb[h] = wq_wide
             w = HID // parts
             cols = slice(part * w, (part + 1) * w)
-            nc.vector.tensor_tensor(out=wide_sb[i][:, cols], in0=raw[i][:, cols].bitcast(FP8), in1=scale_bc[:, cols], op=ALU.mult)
+            nc.vector.tensor_tensor(out=wide_sb[h][:, cols], in0=raw_q[h][:, cols].bitcast(FP8), in1=scale_bc[:, cols], op=ALU.mult)
 
-        def turn_rows(src, grp_w, slot):
+        def turn_x(src, grp_w, slot):
             words = src[:].bitcast(F32)
             for a in range(PASSES // 2):
                 tp = tps.tile([P, 2, 2, P], F32, name="tp")
@@ -161,72 +156,75 @@ def tile_gptneoxattention_pa_kernel(tc, x, wq_bytes, wq_scale, bq, wk, bk, out_0
                         nc.tensor.transpose(out=tp[:, g2, u, :], in_=words[:, 256 * g + u:256 * (g + 1):2], identity=ident[:])
                 nc.scalar.copy(out=grp_w[:, 2 * a:2 * a + 2, slot * P:(slot + 1) * P, :], in_=tp[:].rearrange("p g u r -> p g r u"))
 
-        def turn(i):
-            kind, h = seq[i]
-            grp = grouped.tile([P, PASSES * P * 4], BF16, name="grp", align_bytes=64)
-            grp_sb[i] = grp
-            src = wide_sb[i] if kind == 0 else raw[i]
-            turn_rows(src, grp[:].bitcast(F32).rearrange("p (g c u) -> p g c u", g=PASSES, u=2), 0)
+        def turn(h):
+            grp = grouped.tile([P, 2 * PASSES * P * 4], BF16, name="grp", align_bytes=64)
+            grp_sb[h] = grp
+            grp_w = grp[:].bitcast(F32).rearrange("p (m c u) -> p m c u", m=2 * PASSES, u=2)
+            for kind, src in ((0, wide_sb[h]), (1, raw_k[h])):
+                words = src[:].bitcast(F32)
+                for a in range(PASSES // 2):
+                    tp = tps.tile([P, 2, 2, P], F32, name="tp")
+                    for g2 in range(2):
+                        g = 2 * a + g2
+                        for u in range(2):
+                            nc.tensor.transpose(out=tp[:, u, g2, :], in_=words[:, 256 * g + u:256 * (g + 1):2], identity=ident[:])
+                    nc.scalar.copy(
+                        out=grp_w[:, 4 * a:4 * a + 4, kind * ROT:(kind + 1) * ROT, :],
+                        in_=tp[:].rearrange("p u g (x r) -> p (g x) r u", x=2),
+                    )
 
-        def quantize(i):
-            codes = quant.tile([P, PASSES, P], U32, name="w_codes", align_bytes=64)
-            scl = quant.tile([P, PASSES, P], U8, name="w_scl", align_bytes=64)
+        def quantize(h):
+            codes = quant.tile([P, 2 * PASSES, P], U32, name="w_codes", align_bytes=64)
+            scl = quant.tile([P, 2 * PASSES, P], U8, name="w_scl", align_bytes=64)
             nc.vector.quantize_mx(
-                out=codes[:].rearrange("p g c -> p (g c)").bitcast(FP8X4),
-                scales=scl[:].rearrange("p g c -> p (g c)"),
-                in_=grp_sb[i][:],
+                out=codes[:].rearrange("p m c -> p (m c)").bitcast(FP8X4),
+                scales=scl[:].rearrange("p m c -> p (m c)"),
+                in_=grp_sb[h][:],
             )
-            code_sb[i] = (codes, scl)
+            code_sb[h] = (codes, scl)
 
-        def multiply(i):
-            kind, h = seq[i]
-            codes, scl = code_sb[i]
-            acc = accs.tile([P, TOK], F32, name="acc")
-            for g in range(PASSES):
-                nc.tensor.matmul_mx(
-                    out=acc[:],
-                    lhsT=codes[:, g, :].bitcast(FP8X4),
-                    lhsT_scale=scl[:, g, :],
-                    rhs=x_codes[:, g, :].bitcast(FP8X4),
-                    rhs_scale=x_scl[:, g, :],
-                    start=(g == 0),
-                    stop=(g == PASSES - 1),
-                )
+        def multiply(h):
+            codes, scl = code_sb[h]
+            acc_sb = []
+            for half in range(2):
+                acc = accs.tile([P, TOK], F32, name="acc")
+                acc_sb.append(acc)
+                for g in range(PASSES):
+                    nc.tensor.matmul_mx(
+                        out=acc[:],
+                        lhsT=codes[:, 2 * g + half, :].bitcast(FP8X4),
+                        lhsT_scale=scl[:, 2 * g + half, :],
+                        rhs=x_codes[:, g, :].bitcast(FP8X4),
+                        rhs_scale=x_scl[:, g, :],
+                        start=(g == 0),
+                        stop=(g == PASSES - 1),
+                    )
+            rot_c = chan.tile([P, TOK], F32, name="rot_c")
+            rot_s = chan.tile([P, TOK], F32, name="rot_s")
+            nc.vector.scalar_tensor_tensor(out=rot_c[:], in0=acc_sb[0][:], scalar=bias_col[:, h:h + 1], in1=cos_t[:], op0=ALU.add, op1=ALU.mult)
+            nc.vector.scalar_tensor_tensor(out=rot_s[:], in0=acc_sb[0][:], scalar=bias_col[:, h:h + 1], in1=sin_t[:], op0=ALU.add, op1=ALU.mult)
             by_chan = chan.tile([P, TOK], F32, name="by_chan")
-            col = kind * NH + h
-            nc.scalar.activation(out=by_chan[:], in_=acc[:], func=ACT.Identity, bias=bias_col[:, col:col + 1], scale=1.0)
-            chan_sb[i] = by_chan
+            nc.scalar.activation(out=by_chan[:], in_=acc_sb[1][:], func=ACT.Identity, bias=bias_col[:, NH + h:NH + h + 1], scale=1.0)
+            chan_sb[h] = (rot_c, rot_s, by_chan)
 
-        def turn_back(i):
-            bt = bts.tile([P, B, HD], F32, name="bt")
+        def turn_back(h):
+            rot_c, rot_s, by_chan = chan_sb[h]
+            bt_p = bts.tile([P, B, HD], F32, name="bt")
             for b in range(B):
-                nc.tensor.transpose(out=bt[:, b, :], in_=chan_sb[i][:, b * P:(b + 1) * P], identity=ident[:])
-            back_sb[i] = bt
+                nc.tensor.transpose(out=bt_p[:, b, :], in_=by_chan[:, b * P:(b + 1) * P], identity=ident[:])
+            bt_r = bts.tile([P, B, HD], F32, name="bt")
+            for b in range(B):
+                nc.tensor.matmul(out=bt_r[:, b, :], lhsT=rot_c[:, b * P:(b + 1) * P], rhs=ident[:], is_transpose=True, start=True, stop=False)
+                nc.tensor.matmul(out=bt_r[:, b, :], lhsT=rot_s[:, b * P:(b + 1) * P], rhs=swap[:], is_transpose=True, start=False, stop=True)
+            back_sb[h] = (bt_p, bt_r)
 
-        def finish(pair):
-            res_sb = {}
-            parts = {}
-            for i in pair:
-                res = outp.tile([P, B, HD], F32, name="res")
-                res_sb[i] = res
-                nc.scalar.copy(out=res[:, :, ROT:HD], in_=back_sb[i][:, :, ROT:HD])
-            for i in pair:
-                bt = back_sb[i]
-                part_c = tmp.tile([P, B, ROT], F32, name="part_c")
-                part_s = tmp.tile([P, B, ROT], F32, name="part_s")
-                parts[i] = (part_c, part_s)
-                nc.vector.tensor_tensor(out=part_c[:], in0=bt[:, :, 0:ROT], in1=cos_t[:], op=ALU.mult)
-                nc.vector.tensor_tensor(out=part_s[:], in0=bt[:, :, 0:ROT], in1=sin_t[:], op=ALU.mult)
-            for i in pair:
-                kind, h = seq[i]
-                nc.vector.tensor_tensor(
-                    out=res_sb[i][:, :, 0:ROT].rearrange("p b (j e) -> p b j e", e=2),
-                    in0=parts[i][0][:].rearrange("p b (j e) -> p b j e", e=2),
-                    in1=parts[i][1][:].rearrange("p b (j e) -> p b j e", e=2)[:, :, :, ::-1],
-                    op=ALU.add,
-                )
-                dst = out_0 if kind == 0 else out_1
-                nc.sync.dma_start(out=dst[:, h, :, :].rearrange("b s d -> s b d"), in_=res_sb[i][:])
+        def finish(h):
+            bt_p, bt_r = back_sb[h]
+            res = outp.tile([P, 2, B, HD], F32, name="res")
+            nc.scalar.copy(out=res[:, :, :, ROT:HD].rearrange("p k b r -> p b k r"), in_=bt_p[:].rearrange("p b (k r) -> p b k r", k=2))
+            nc.scalar.copy(out=res[:, :, :, 0:ROT].rearrange("p k b r -> p b k r"), in_=bt_r[:].rearrange("p b (k r) -> p b k r", k=2))
+            nc.sync.dma_start(out=out_0[:, h, :, :].rearrange("b s d -> s b d"), in_=res[:, 0, :, :])
+            nc.sync.dma_start(out=out_1[:, h, :, :].rearrange("b s d -> s b d"), in_=res[:, 1, :, :])
 
         bias_f = const.tile([P, P], F32)
         nc.vector.tensor_copy(out=bias_f[:], in_=bias_rows[:])
@@ -236,17 +234,18 @@ def tile_gptneoxattention_pa_kernel(tc, x, wq_bytes, wq_scale, bq, wk, bk, out_0
             widen(0, part, 4)
         bias_col = const.tile([P, 2 * NH], F32)
         nc.vector.tensor_copy(out=bias_col[:], in_=bias_ps[:, 0, 0, 0:2 * NH])
-        for b in range(B):
-            nc.vector.tensor_copy(out=cos_t[:, b, :], in_=table[:, 0:ROT])
-            nc.vector.tensor_copy(out=sin_t[:, b, :], in_=table[:, ROT:2 * ROT])
-        widen(2, 0, 1)
-        turn(0)
+        swap = const.tile([P, P], F32)
+        nc.vector.tensor_copy(
+            out=swap[:].rearrange("p (j e) -> p j e", e=2),
+            in_=ident[:].rearrange("p (j e) -> p j e", e=2)[:, :, ::-1],
+        )
+        widen(1, 0, 1)
         xg = const.tile([P, PASSES * TOK * 4], BF16, align_bytes=64)
         xg_w = xg[:].bitcast(F32).rearrange("p (g c u) -> p g c u", g=PASSES, u=2)
         x_codes = const.tile([P, PASSES, TOK], U32, align_bytes=64)
         x_scl = const.tile([P, PASSES, TOK], U8, align_bytes=64)
         for b in range(B):
-            turn_rows(x_raw[b], xg_w, b)
+            turn_x(x_raw[b], xg_w, b)
             for g in range(PASSES):
                 first = (g * TOK + b * P) * 4
                 nc.vector.quantize_mx(
@@ -254,23 +253,25 @@ def tile_gptneoxattention_pa_kernel(tc, x, wq_bytes, wq_scale, bq, wk, bk, out_0
                     scales=x_scl[:, g, b * P:(b + 1) * P],
                     in_=xg[:, first:first + 4 * P],
                 )
-        turn(1)
+        turn(0)
         quantize(0)
-        quantize(1)
+        cos_t = const.tile([P, TOK], F32)
+        sin_t = const.tile([P, TOK], F32)
+        for c, dst in ((0, cos_t), (1, sin_t)):
+            tab_ps = tps.tile([P, 2, 2, P], F32, name="tp")
+            for a in range(2):
+                for u in range(2):
+                    nc.tensor.transpose(out=tab_ps[:, a, u, :], in_=table[:, c, :, :].rearrange("p k r -> p (k r)"), identity=ident[:])
+            nc.scalar.copy(out=dst[:], in_=tab_ps[:].rearrange("p a u r -> p (a u r)"))
 
-        n_pairs = n_heads // 2
-        for j in range(n_pairs + 1):
-            if j + 2 < n_pairs:
-                widen(2 * (j + 2), 0, 1)
-            if j + 1 < n_pairs:
-                turn(2 * j + 2)
-                turn(2 * j + 3)
-                quantize(2 * j + 2)
-                quantize(2 * j + 3)
+        for j in range(NH + 1):
+            if j + 2 < NH:
+                widen(j + 2, 0, 1)
+            if j + 1 < NH:
+                turn(j + 1)
+                quantize(j + 1)
             if j >= 1:
-                turn_back(2 * j - 2)
-                turn_back(2 * j - 1)
-                finish((2 * j - 2, 2 * j - 1))
-            if j < n_pairs:
-                multiply(2 * j)
-                multiply(2 * j + 1)
+                turn_back(j - 1)
+                finish(j - 1)
+            if j < NH:
+                multiply(j)

@@ -32,8 +32,9 @@ def tile_gptneoxattention_pa_kernel(tc, x, wq_bytes, wq_scale, bq, wk, bk, out_0
         wide = ctx.enter_context(tc.tile_pool(name="wide", bufs=3))
         grouped = ctx.enter_context(tc.tile_pool(name="grouped", bufs=2))
         quant = ctx.enter_context(tc.tile_pool(name="quant", bufs=3))
-        chan = ctx.enter_context(tc.tile_pool(name="chan", bufs=2))
+        chan = ctx.enter_context(tc.tile_pool(name="chan", bufs=4))
         outp = ctx.enter_context(tc.tile_pool(name="outp", bufs=3))
+        tmp = ctx.enter_context(tc.tile_pool(name="tmp", bufs=2))
         tps = ctx.enter_context(tc.psum_pool(name="tps", bufs=4))
         accs = ctx.enter_context(tc.psum_pool(name="accs", bufs=2))
         bts = ctx.enter_context(tc.psum_pool(name="bts", bufs=2))
@@ -75,12 +76,10 @@ def tile_gptneoxattention_pa_kernel(tc, x, wq_bytes, wq_scale, bq, wk, bk, out_0
             for half in range(2):
                 nc.sync.dma_start(out=bias_rows[half * NH:(half + 1) * NH, kind * ROT:(kind + 1) * ROT], in_=halves[half])
         load_q(0)
-        load_q(1)
         for b in range(B):
             load_x(b)
         load_k(0)
-        load_k(1)
-        for h in range(2, NH):
+        for h in range(1, NH):
             load_q(h)
             load_k(h)
 
@@ -128,15 +127,18 @@ def tile_gptneoxattention_pa_kernel(tc, x, wq_bytes, wq_scale, bq, wk, bk, out_0
         nc.vector.tensor_single_scalar(out=under[:], in_=red3[:], scalar=-math.pi, op=ALU.is_lt)
         red4 = const.tile([P, 2 * ROT], F32)
         nc.vector.scalar_tensor_tensor(out=red4[:], in0=under[:], scalar=2.0 * math.pi, in1=red3[:], op0=ALU.mult, op1=ALU.add)
-        table = const.tile([P, 2, 2, ROT], F32)
-        for kind in range(2):
-            nc.scalar.activation(out=table[:, :, kind, :], in_=red4[:].rearrange("p (c r) -> p c r", c=2), func=ACT.Sin)
+        table = const.tile([P, 2, 2 * B, ROT], F32)
+        for n in range(2 * B):
+            nc.scalar.activation(out=table[:, :, n, :], in_=red4[:].rearrange("p (c r) -> p c r", c=2), func=ACT.Sin)
+        cos_t = table[:, 0, :, :]
+        sin_t = table[:, 1, :, :]
 
         wide_sb = {}
         grp_sb = {}
         code_sb = {}
         chan_sb = {}
         back_sb = {}
+        res_sb = {}
 
         def widen(h, part, parts):
             if part == 0:
@@ -156,22 +158,23 @@ def tile_gptneoxattention_pa_kernel(tc, x, wq_bytes, wq_scale, bq, wk, bk, out_0
                         nc.tensor.transpose(out=tp[:, g2, u, :], in_=words[:, 256 * g + u:256 * (g + 1):2], identity=ident[:])
                 nc.scalar.copy(out=grp_w[:, 2 * a:2 * a + 2, slot * P:(slot + 1) * P, :], in_=tp[:].rearrange("p g u r -> p g r u"))
 
-        def turn(h):
-            grp = grouped.tile([P, 2 * PASSES * P * 4], BF16, name="grp", align_bytes=64)
-            grp_sb[h] = grp
-            grp_w = grp[:].bitcast(F32).rearrange("p (m c u) -> p m c u", m=2 * PASSES, u=2)
-            for kind, src in ((0, wide_sb[h]), (1, raw_k[h])):
-                words = src[:].bitcast(F32)
-                for a in range(PASSES // 2):
-                    tp = tps.tile([P, 2, 2, P], F32, name="tp")
-                    for g2 in range(2):
-                        g = 2 * a + g2
-                        for u in range(2):
-                            nc.tensor.transpose(out=tp[:, u, g2, :], in_=words[:, 256 * g + u:256 * (g + 1):2], identity=ident[:])
-                    nc.scalar.copy(
-                        out=grp_w[:, 4 * a:4 * a + 4, kind * ROT:(kind + 1) * ROT, :],
-                        in_=tp[:].rearrange("p u g (x r) -> p (g x) r u", x=2),
-                    )
+        def turn(h, kind):
+            if h not in grp_sb:
+                grp = grouped.tile([P, 2 * PASSES * P * 4], BF16, name="grp", align_bytes=64)
+                grp_sb[h] = grp
+            grp_w = grp_sb[h][:].bitcast(F32).rearrange("p (m c u) -> p m c u", m=2 * PASSES, u=2)
+            src = wide_sb[h] if kind == 0 else raw_k[h]
+            words = src[:].bitcast(F32)
+            for a in range(PASSES // 2):
+                tp = tps.tile([P, 2, 2, P], F32, name="tp")
+                for g2 in range(2):
+                    g = 2 * a + g2
+                    for u in range(2):
+                        nc.tensor.transpose(out=tp[:, u, g2, :], in_=words[:, 256 * g + u:256 * (g + 1):2], identity=ident[:])
+                nc.scalar.copy(
+                    out=grp_w[:, 4 * a:4 * a + 4, kind * ROT:(kind + 1) * ROT, :],
+                    in_=tp[:].rearrange("p u g (x r) -> p (g x) r u", x=2),
+                )
 
         def quantize(h):
             codes = quant.tile([P, 2 * PASSES, P], U32, name="w_codes", align_bytes=64)
@@ -183,63 +186,62 @@ def tile_gptneoxattention_pa_kernel(tc, x, wq_bytes, wq_scale, bq, wk, bk, out_0
             )
             code_sb[h] = (codes, scl)
 
-        def multiply(h):
+        def multiply(h, half):
             codes, scl = code_sb[h]
-            acc_sb = []
-            for half in range(2):
-                acc = accs.tile([P, TOK], F32, name="acc")
-                acc_sb.append(acc)
-                for g in range(PASSES):
-                    nc.tensor.matmul_mx(
-                        out=acc[:],
-                        lhsT=codes[:, 2 * g + half, :].bitcast(FP8X4),
-                        lhsT_scale=scl[:, 2 * g + half, :],
-                        rhs=x_codes[:, g, :].bitcast(FP8X4),
-                        rhs_scale=x_scl[:, g, :],
-                        start=(g == 0),
-                        stop=(g == PASSES - 1),
-                    )
-            rot_c = chan.tile([P, TOK], F32, name="rot_c")
-            rot_s = chan.tile([P, TOK], F32, name="rot_s")
-            nc.vector.scalar_tensor_tensor(out=rot_c[:], in0=acc_sb[0][:], scalar=bias_col[:, h:h + 1], in1=cos_t[:], op0=ALU.add, op1=ALU.mult)
-            nc.vector.scalar_tensor_tensor(out=rot_s[:], in0=acc_sb[0][:], scalar=bias_col[:, h:h + 1], in1=sin_t[:], op0=ALU.add, op1=ALU.mult)
+            acc = accs.tile([P, TOK], F32, name="acc")
+            for g in range(PASSES):
+                nc.tensor.matmul_mx(
+                    out=acc[:],
+                    lhsT=codes[:, 2 * g + half, :].bitcast(FP8X4),
+                    lhsT_scale=scl[:, 2 * g + half, :],
+                    rhs=x_codes[:, g, :].bitcast(FP8X4),
+                    rhs_scale=x_scl[:, g, :],
+                    start=(g == 0),
+                    stop=(g == PASSES - 1),
+                )
             by_chan = chan.tile([P, TOK], F32, name="by_chan")
-            nc.scalar.activation(out=by_chan[:], in_=acc_sb[1][:], func=ACT.Identity, bias=bias_col[:, NH + h:NH + h + 1], scale=1.0)
-            chan_sb[h] = (rot_c, rot_s, by_chan)
+            col = half * NH + h
+            nc.scalar.activation(out=by_chan[:], in_=acc[:], func=ACT.Identity, bias=bias_col[:, col:col + 1], scale=1.0)
+            chan_sb[(h, half)] = by_chan
 
-        def turn_back(h):
-            rot_c, rot_s, by_chan = chan_sb[h]
-            bt_p = bts.tile([P, B, HD], F32, name="bt")
+        def turn_back(h, half):
+            bt = bts.tile([P, B, HD], F32, name="bt")
             for b in range(B):
-                nc.tensor.transpose(out=bt_p[:, b, :], in_=by_chan[:, b * P:(b + 1) * P], identity=ident[:])
-            bt_r = bts.tile([P, B, HD], F32, name="bt")
-            for b in range(B):
-                nc.tensor.matmul(out=bt_r[:, b, :], lhsT=rot_c[:, b * P:(b + 1) * P], rhs=ident[:], is_transpose=True, start=True, stop=False)
-                nc.tensor.matmul(out=bt_r[:, b, :], lhsT=rot_s[:, b * P:(b + 1) * P], rhs=swap[:], is_transpose=True, start=False, stop=True)
-            back_sb[h] = (bt_p, bt_r)
+                nc.tensor.transpose(out=bt[:, b, :], in_=chan_sb[(h, half)][:, b * P:(b + 1) * P], identity=ident[:])
+            back_sb[(h, half)] = bt
+
+        def rotate(h):
+            bt = back_sb[(h, 0)][:].rearrange("p b (k r) -> p (b k) r", k=2)
+            res = outp.tile([P, B, 2, HD], F32, name="res")
+            res_sb[h] = res
+            part_c = tmp.tile([P, 2 * B, ROT], F32, name="part_c")
+            part_s = tmp.tile([P, 2 * B, ROT], F32, name="part_s")
+            nc.vector.tensor_tensor(out=part_c[:], in0=bt, in1=cos_t, op=ALU.mult)
+            nc.vector.tensor_tensor(out=part_s[:], in0=bt, in1=sin_t, op=ALU.mult)
+            nc.vector.tensor_tensor(
+                out=res[:, :, :, 0:ROT].rearrange("p b k (j e) -> p (b k) j e", e=2),
+                in0=part_c[:].rearrange("p n (j e) -> p n j e", e=2),
+                in1=part_s[:].rearrange("p n (j e) -> p n j e", e=2)[:, :, :, ::-1],
+                op=ALU.add,
+            )
 
         def finish(h):
-            bt_p, bt_r = back_sb[h]
-            res = outp.tile([P, 2, B, HD], F32, name="res")
-            nc.scalar.copy(out=res[:, :, :, ROT:HD].rearrange("p k b r -> p b k r"), in_=bt_p[:].rearrange("p b (k r) -> p b k r", k=2))
-            nc.scalar.copy(out=res[:, :, :, 0:ROT].rearrange("p k b r -> p b k r"), in_=bt_r[:].rearrange("p b (k r) -> p b k r", k=2))
-            nc.sync.dma_start(out=out_0[:, h, :, :].rearrange("b s d -> s b d"), in_=res[:, 0, :, :])
-            nc.sync.dma_start(out=out_1[:, h, :, :].rearrange("b s d -> s b d"), in_=res[:, 1, :, :])
+            res = res_sb[h]
+            nc.scalar.copy(
+                out=res[:, :, :, ROT:HD].rearrange("p b k r -> p (b k) r"),
+                in_=back_sb[(h, 1)][:].rearrange("p b (k r) -> p (b k) r", k=2),
+            )
+            nc.sync.dma_start(out=out_0[:, h, :, :].rearrange("b s d -> s b d"), in_=res[:, :, 0, :])
+            nc.sync.dma_start(out=out_1[:, h, :, :].rearrange("b s d -> s b d"), in_=res[:, :, 1, :])
 
         bias_f = const.tile([P, P], F32)
         nc.vector.tensor_copy(out=bias_f[:], in_=bias_rows[:])
         bias_ps = tps.tile([P, 2, 2, P], F32, name="tp")
         nc.tensor.transpose(out=bias_ps[:, 0, 0, :], in_=bias_f[:], identity=ident[:])
+        bias_col = const.tile([P, 2 * NH], F32)
+        nc.scalar.copy(out=bias_col[:], in_=bias_ps[:, 0, 0, 0:2 * NH])
         for part in range(4):
             widen(0, part, 4)
-        bias_col = const.tile([P, 2 * NH], F32)
-        nc.vector.tensor_copy(out=bias_col[:], in_=bias_ps[:, 0, 0, 0:2 * NH])
-        swap = const.tile([P, P], F32)
-        nc.vector.tensor_copy(
-            out=swap[:].rearrange("p (j e) -> p j e", e=2),
-            in_=ident[:].rearrange("p (j e) -> p j e", e=2)[:, :, ::-1],
-        )
-        widen(1, 0, 1)
         xg = const.tile([P, PASSES * TOK * 4], BF16, align_bytes=64)
         xg_w = xg[:].bitcast(F32).rearrange("p (g c u) -> p g c u", g=PASSES, u=2)
         x_codes = const.tile([P, PASSES, TOK], U32, align_bytes=64)
@@ -253,25 +255,26 @@ def tile_gptneoxattention_pa_kernel(tc, x, wq_bytes, wq_scale, bq, wk, bk, out_0
                     scales=x_scl[:, g, b * P:(b + 1) * P],
                     in_=xg[:, first:first + 4 * P],
                 )
-        turn(0)
+        widen(1, 0, 1)
+        turn(0, 0)
+        turn(0, 1)
         quantize(0)
-        cos_t = const.tile([P, TOK], F32)
-        sin_t = const.tile([P, TOK], F32)
-        for c, dst in ((0, cos_t), (1, sin_t)):
-            tab_ps = tps.tile([P, 2, 2, P], F32, name="tp")
-            for a in range(2):
-                for u in range(2):
-                    nc.tensor.transpose(out=tab_ps[:, a, u, :], in_=table[:, c, :, :].rearrange("p k r -> p (k r)"), identity=ident[:])
-            nc.scalar.copy(out=dst[:], in_=tab_ps[:].rearrange("p a u r -> p (a u r)"))
 
         for j in range(NH + 1):
+            if j + 1 < NH:
+                turn(j + 1, 1)
+            if j >= 1:
+                turn_back(j - 1, 0)
+                rotate(j - 1)
+            if j < NH:
+                multiply(j, 0)
             if j + 2 < NH:
                 widen(j + 2, 0, 1)
             if j + 1 < NH:
-                turn(j + 1)
+                turn(j + 1, 0)
                 quantize(j + 1)
             if j >= 1:
-                turn_back(j - 1)
+                turn_back(j - 1, 1)
                 finish(j - 1)
             if j < NH:
-                multiply(j)
+                multiply(j, 1)

@@ -20,6 +20,7 @@ PASSES = HID // 512
 TOK = SEQ * B
 ROT = 2 * RD
 FLOPS = 2 * SEQ * B * HID * 2 * NH * HD
+AHEAD = 5
 
 
 def tile_gptneoxattention_pa_kernel(tc, x, wq_bytes, wq_scale, bq, wk, bk, out_0, out_1):
@@ -79,7 +80,7 @@ def tile_gptneoxattention_pa_kernel(tc, x, wq_bytes, wq_scale, bq, wk, bk, out_0
         for b in range(B):
             load_x(b)
         load_k(0)
-        for h in range(1, NH):
+        for h in range(1, AHEAD):
             load_q(h)
             load_k(h)
 
@@ -261,6 +262,9 @@ def tile_gptneoxattention_pa_kernel(tc, x, wq_bytes, wq_scale, bq, wk, bk, out_0
         quantize(0)
 
         for j in range(NH + 1):
+            if j + AHEAD < NH:
+                load_q(j + AHEAD)
+                load_k(j + AHEAD)
             if j + 1 < NH:
                 turn(j + 1, 1)
             if j >= 1:

@@ -20,7 +20,7 @@ PASSES = HID // 512
 TOK = SEQ * B
 ROT = 2 * RD
 FLOPS = 2 * SEQ * B * HID * 2 * NH * HD
-AHEAD = 5
+AHEAD = 6
 
 
 def tile_gptneoxattention_pa_kernel(tc, x, wq_bytes, wq_scale, bq, wk, bk, out_0, out_1):
@@ -28,11 +28,11 @@ def tile_gptneoxattention_pa_kernel(tc, x, wq_bytes, wq_scale, bq, wk, bk, out_0
     with ExitStack() as ctx:
         ctx.enter_context(tc.manual_schedule())
         const = ctx.enter_context(tc.tile_pool(name="const", bufs=1))
-        rows = ctx.enter_context(tc.tile_pool(name="rows", bufs=16))
-        qbytes = ctx.enter_context(tc.tile_pool(name="qbytes", bufs=16))
+        rows = ctx.enter_context(tc.tile_pool(name="rows", bufs=12))
+        qbytes = ctx.enter_context(tc.tile_pool(name="qbytes", bufs=8))
         wide = ctx.enter_context(tc.tile_pool(name="wide", bufs=3))
-        grouped = ctx.enter_context(tc.tile_pool(name="grouped", bufs=2))
-        quant = ctx.enter_context(tc.tile_pool(name="quant", bufs=3))
+        grouped = ctx.enter_context(tc.tile_pool(name="grouped", bufs=3))
+        quant = ctx.enter_context(tc.tile_pool(name="quant", bufs=4))
         chan = ctx.enter_context(tc.tile_pool(name="chan", bufs=4))
         outp = ctx.enter_context(tc.tile_pool(name="outp", bufs=3))
         tmp = ctx.enter_context(tc.tile_pool(name="tmp", bufs=2))
@@ -129,8 +129,6 @@ def tile_gptneoxattention_pa_kernel(tc, x, wq_bytes, wq_scale, bq, wk, bk, out_0
         red4 = const.tile([P, 2 * ROT], F32)
         nc.vector.scalar_tensor_tensor(out=red4[:], in0=under[:], scalar=2.0 * math.pi, in1=red3[:], op0=ALU.mult, op1=ALU.add)
         table = const.tile([P, 2, 2 * B, ROT], F32)
-        for n in range(2 * B):
-            nc.scalar.activation(out=table[:, :, n, :], in_=red4[:].rearrange("p (c r) -> p c r", c=2), func=ACT.Sin)
         cos_t = table[:, 0, :, :]
         sin_t = table[:, 1, :, :]
 
@@ -260,23 +258,29 @@ def tile_gptneoxattention_pa_kernel(tc, x, wq_bytes, wq_scale, bq, wk, bk, out_0
         turn(0, 0)
         turn(0, 1)
         quantize(0)
+        widen(2, 0, 1)
+        turn(1, 1)
+        turn(1, 0)
+        quantize(1)
+        for n in range(2 * B):
+            nc.scalar.activation(out=table[:, :, n, :], in_=red4[:].rearrange("p (c r) -> p c r", c=2), func=ACT.Sin)
 
         for j in range(NH + 1):
             if j + AHEAD < NH:
                 load_q(j + AHEAD)
                 load_k(j + AHEAD)
-            if j + 1 < NH:
-                turn(j + 1, 1)
+            if j + 2 < NH:
+                turn(j + 2, 1)
             if j >= 1:
                 turn_back(j - 1, 0)
                 rotate(j - 1)
             if j < NH:
                 multiply(j, 0)
+            if j + 3 < NH:
+                widen(j + 3, 0, 1)
             if j + 2 < NH:
-                widen(j + 2, 0, 1)
-            if j + 1 < NH:
-                turn(j + 1, 0)
-                quantize(j + 1)
+                turn(j + 2, 0)
+                quantize(j + 2)
             if j >= 1:
                 turn_back(j - 1, 1)
                 finish(j - 1)

@@ -21,6 +21,7 @@ TOK = SEQ * B
 ROT = 2 * RD
 FLOPS = 2 * SEQ * B * HID * 2 * NH * HD
 AHEAD = 6
+SORT_FROM = 3
 
 
 def tile_gptneoxattention_pa_kernel(tc, x, wq_bytes, wq_scale, bq, wk, bk, out_0, out_1):
@@ -31,6 +32,7 @@ def tile_gptneoxattention_pa_kernel(tc, x, wq_bytes, wq_scale, bq, wk, bk, out_0
         rows = ctx.enter_context(tc.tile_pool(name="rows", bufs=12))
         qbytes = ctx.enter_context(tc.tile_pool(name="qbytes", bufs=8))
         wide = ctx.enter_context(tc.tile_pool(name="wide", bufs=3))
+        sorted_k = ctx.enter_context(tc.tile_pool(name="sorted_k", bufs=3))
         grouped = ctx.enter_context(tc.tile_pool(name="grouped", bufs=3))
         quant = ctx.enter_context(tc.tile_pool(name="quant", bufs=4))
         chan = ctx.enter_context(tc.tile_pool(name="chan", bufs=4))
@@ -138,6 +140,8 @@ def tile_gptneoxattention_pa_kernel(tc, x, wq_bytes, wq_scale, bq, wk, bk, out_0
         chan_sb = {}
         back_sb = {}
         res_sb = {}
+        sort_sb = {}
+        part_sb = {}
 
         def widen(h, part, parts):
             if part == 0:
@@ -146,6 +150,14 @@ def tile_gptneoxattention_pa_kernel(tc, x, wq_bytes, wq_scale, bq, wk, bk, out_0
             w = HID // parts
             cols = slice(part * w, (part + 1) * w)
             nc.vector.tensor_tensor(out=wide_sb[h][:, cols], in0=raw_q[h][:, cols].bitcast(FP8), in1=scale_bc[:, cols], op=ALU.mult)
+
+        def sort_words(h):
+            wk_sorted = sorted_k.tile([P, HID // 2], BF16, name="wk_sorted")
+            sort_sb[h] = wk_sorted
+            nc.scalar.copy(
+                out=wk_sorted[:].bitcast(F32).rearrange("p (g u c) -> p g u c", g=PASSES // 2, u=2),
+                in_=raw_k[h][:, 0:HID // 2].bitcast(F32).rearrange("p (g c u) -> p g u c", g=PASSES // 2, u=2),
+            )
 
         def turn_x(src, grp_w, slot):
             words = src[:].bitcast(F32)
@@ -169,7 +181,11 @@ def tile_gptneoxattention_pa_kernel(tc, x, wq_bytes, wq_scale, bq, wk, bk, out_0
                 for g2 in range(2):
                     g = 2 * a + g2
                     for u in range(2):
-                        nc.tensor.transpose(out=tp[:, u, g2, :], in_=words[:, 256 * g + u:256 * (g + 1):2], identity=ident[:])
+                        if kind == 1 and a == 0 and h in sort_sb:
+                            first = 256 * g + P * u
+                            nc.tensor.transpose(out=tp[:, u, g2, :], in_=sort_sb[h][:].bitcast(F32)[:, first:first + P], identity=ident[:])
+                        else:
+                            nc.tensor.transpose(out=tp[:, u, g2, :], in_=words[:, 256 * g + u:256 * (g + 1):2], identity=ident[:])
                 nc.scalar.copy(
                     out=grp_w[:, 4 * a:4 * a + 4, kind * ROT:(kind + 1) * ROT, :],
                     in_=tp[:].rearrange("p u g (x r) -> p (g x) r u", x=2),
@@ -209,14 +225,18 @@ def tile_gptneoxattention_pa_kernel(tc, x, wq_bytes, wq_scale, bq, wk, bk, out_0
                 nc.tensor.transpose(out=bt[:, b, :], in_=chan_sb[(h, half)][:, b * P:(b + 1) * P], identity=ident[:])
             back_sb[(h, half)] = bt
 
-        def rotate(h):
+        def rotary_products(h):
             bt = back_sb[(h, 0)][:].rearrange("p b (k r) -> p (b k) r", k=2)
-            res = outp.tile([P, B, 2, HD], F32, name="res")
-            res_sb[h] = res
             part_c = tmp.tile([P, 2 * B, ROT], F32, name="part_c")
             part_s = tmp.tile([P, 2 * B, ROT], F32, name="part_s")
+            part_sb[h] = (part_c, part_s)
             nc.vector.tensor_tensor(out=part_c[:], in0=bt, in1=cos_t, op=ALU.mult)
             nc.vector.tensor_tensor(out=part_s[:], in0=bt, in1=sin_t, op=ALU.mult)
+
+        def rotary_add(h):
+            part_c, part_s = part_sb[h]
+            res = outp.tile([P, B, 2, HD], F32, name="res")
+            res_sb[h] = res
             nc.vector.tensor_tensor(
                 out=res[:, :, :, 0:ROT].rearrange("p b k (j e) -> p (b k) j e", e=2),
                 in0=part_c[:].rearrange("p n (j e) -> p n j e", e=2),
@@ -271,13 +291,17 @@ def tile_gptneoxattention_pa_kernel(tc, x, wq_bytes, wq_scale, bq, wk, bk, out_0
                 load_k(j + AHEAD)
             if j + 2 < NH:
                 turn(j + 2, 1)
+            if SORT_FROM <= j + 3 < NH:
+                sort_words(j + 3)
             if j >= 1:
                 turn_back(j - 1, 0)
-                rotate(j - 1)
+                rotary_products(j - 1)
             if j < NH:
                 multiply(j, 0)
             if j + 3 < NH:
                 widen(j + 3, 0, 1)
+            if j >= 1:
+                rotary_add(j - 1)
             if j + 2 < NH:
                 turn(j + 2, 0)
                 quantize(j + 2)

@@ -33,6 +33,7 @@ def tile_gptneoxattention_pa_kernel(tc, x, wq_bytes, wq_scale, bq, wk, bk, out_0
         qbytes = ctx.enter_context(tc.tile_pool(name="qbytes", bufs=8))
         wide = ctx.enter_context(tc.tile_pool(name="wide", bufs=3))
         sorted_k = ctx.enter_context(tc.tile_pool(name="sorted_k", bufs=3))
+        sorted_q = ctx.enter_context(tc.tile_pool(name="sorted_q", bufs=2))
         grouped = ctx.enter_context(tc.tile_pool(name="grouped", bufs=3))
         quant = ctx.enter_context(tc.tile_pool(name="quant", bufs=4))
         chan = ctx.enter_context(tc.tile_pool(name="chan", bufs=4))
@@ -141,6 +142,7 @@ def tile_gptneoxattention_pa_kernel(tc, x, wq_bytes, wq_scale, bq, wk, bk, out_0
         back_sb = {}
         res_sb = {}
         sort_sb = {}
+        sort_q_sb = {}
         part_sb = {}
 
         def widen(h, part, parts):
@@ -157,6 +159,14 @@ def tile_gptneoxattention_pa_kernel(tc, x, wq_bytes, wq_scale, bq, wk, bk, out_0
             nc.scalar.copy(
                 out=wk_sorted[:].bitcast(F32).rearrange("p (g u c) -> p g u c", g=PASSES // 2, u=2),
                 in_=raw_k[h][:, 0:HID // 2].bitcast(F32).rearrange("p (g c u) -> p g u c", g=PASSES // 2, u=2),
+            )
+
+        def sort_last_pass(h):
+            wq_sorted = sorted_q.tile([P, 512], BF16, name="wq_sorted")
+            sort_q_sb[h] = wq_sorted
+            nc.scalar.copy(
+                out=wq_sorted[:].bitcast(F32).rearrange("p (u c) -> p u c", u=2),
+                in_=wide_sb[h][:, HID - 512:HID].bitcast(F32).rearrange("p (c u) -> p u c", u=2),
             )
 
         def turn_x(src, grp_w, slot):
@@ -184,6 +194,8 @@ def tile_gptneoxattention_pa_kernel(tc, x, wq_bytes, wq_scale, bq, wk, bk, out_0
                         if kind == 1 and a == 0 and h in sort_sb:
                             first = 256 * g + P * u
                             nc.tensor.transpose(out=tp[:, u, g2, :], in_=sort_sb[h][:].bitcast(F32)[:, first:first + P], identity=ident[:])
+                        elif kind == 0 and g == PASSES - 1 and h in sort_q_sb:
+                            nc.tensor.transpose(out=tp[:, u, g2, :], in_=sort_q_sb[h][:].bitcast(F32)[:, P * u:P * (u + 1)], identity=ident[:])
                         else:
                             nc.tensor.transpose(out=tp[:, u, g2, :], in_=words[:, 256 * g + u:256 * (g + 1):2], identity=ident[:])
                 nc.scalar.copy(
@@ -226,12 +238,12 @@ def tile_gptneoxattention_pa_kernel(tc, x, wq_bytes, wq_scale, bq, wk, bk, out_0
             back_sb[(h, half)] = bt
 
         def rotary_products(h):
-            bt = back_sb[(h, 0)][:].rearrange("p b (k r) -> p (b k) r", k=2)
-            part_c = tmp.tile([P, 2 * B, ROT], F32, name="part_c")
-            part_s = tmp.tile([P, 2 * B, ROT], F32, name="part_s")
-            part_sb[h] = (part_c, part_s)
-            nc.vector.tensor_tensor(out=part_c[:], in0=bt, in1=cos_t, op=ALU.mult)
-            nc.vector.tensor_tensor(out=part_s[:], in0=bt, in1=sin_t, op=ALU.mult)
+            bt = back_sb[(h, 0)][:].rearrange("p b c -> p (b c)").unsqueeze(1).to_broadcast([P, 2, TOK])
+            parts = tmp.tile([P, 2, 2 * B, ROT], F32, name="parts")
+            part_sb[h] = (parts[:, 0, :, :], parts[:, 1, :, :])
+            nc.vector.tensor_tensor(
+                out=parts[:].rearrange("p c n r -> p c (n r)"), in0=bt, in1=table[:].rearrange("p c n r -> p c (n r)"), op=ALU.mult
+            )
 
         def rotary_add(h):
             part_c, part_s = part_sb[h]
@@ -239,8 +251,8 @@ def tile_gptneoxattention_pa_kernel(tc, x, wq_bytes, wq_scale, bq, wk, bk, out_0
             res_sb[h] = res
             nc.vector.tensor_tensor(
                 out=res[:, :, :, 0:ROT].rearrange("p b k (j e) -> p (b k) j e", e=2),
-                in0=part_c[:].rearrange("p n (j e) -> p n j e", e=2),
-                in1=part_s[:].rearrange("p n (j e) -> p n j e", e=2)[:, :, :, ::-1],
+                in0=part_c.rearrange("p n (j e) -> p n j e", e=2),
+                in1=part_s.rearrange("p n (j e) -> p n j e", e=2)[:, :, :, ::-1],
                 op=ALU.add,
             )
 
@@ -267,14 +279,13 @@ def tile_gptneoxattention_pa_kernel(tc, x, wq_bytes, wq_scale, bq, wk, bk, out_0
         x_scl = const.tile([P, PASSES, TOK], U8, align_bytes=64)
         for b in range(B):
             turn_x(x_raw[b], xg_w, b)
-            for g in range(PASSES):
-                first = (g * TOK + b * P) * 4
-                nc.vector.quantize_mx(
-                    out=x_codes[:, g, b * P:(b + 1) * P].bitcast(FP8X4),
-                    scales=x_scl[:, g, b * P:(b + 1) * P],
-                    in_=xg[:, first:first + 4 * P],
-                )
         widen(1, 0, 1)
+        for g in range(PASSES):
+            nc.vector.quantize_mx(
+                out=x_codes[:, g, :].bitcast(FP8X4),
+                scales=x_scl[:, g, :],
+                in_=xg[:, g * TOK * 4:(g + 1) * TOK * 4],
+            )
         turn(0, 0)
         turn(0, 1)
         quantize(0)
@@ -291,6 +302,8 @@ def tile_gptneoxattention_pa_kernel(tc, x, wq_bytes, wq_scale, bq, wk, bk, out_0
                 load_k(j + AHEAD)
             if j + 2 < NH:
                 turn(j + 2, 1)
+            if SORT_FROM <= j + 2 < NH:
+                sort_last_pass(j + 2)
             if SORT_FROM <= j + 3 < NH:
                 sort_words(j + 3)
             if j >= 1:

@@ -80,10 +80,15 @@ def tile_gptneoxattention_pa_kernel(tc, x, wq_bytes, wq_scale, bq, wk, bk, out_0
             for half in range(2):
                 nc.sync.dma_start(out=bias_rows[half * NH:(half + 1) * NH, kind * ROT:(kind + 1) * ROT], in_=halves[half])
         load_q(0)
-        for b in range(B):
-            load_x(b)
-        load_k(0)
-        for h in range(1, AHEAD):
+        load_x(0)
+        load_x(1)
+        load_q(1)
+        load_x(2)
+        load_x(3)
+        load_q(2)
+        for h in range(3):
+            load_k(h)
+        for h in range(3, AHEAD):
             load_q(h)
             load_k(h)
 
@@ -213,29 +218,33 @@ def tile_gptneoxattention_pa_kernel(tc, x, wq_bytes, wq_scale, bq, wk, bk, out_0
             )
             code_sb[h] = (codes, scl)
 
-        def multiply(h, half):
+        def multiply(h, half, first=0, last=B):
             codes, scl = code_sb[h]
-            acc = accs.tile([P, TOK], F32, name="acc")
+            if first == 0:
+                acc = accs.tile([P, TOK], F32, name="acc")
+                by_chan = chan.tile([P, TOK], F32, name="by_chan")
+                chan_sb[(h, half)] = (acc, by_chan)
+            acc, by_chan = chan_sb[(h, half)]
+            cols = slice(first * P, last * P)
             for g in range(PASSES):
                 nc.tensor.matmul_mx(
-                    out=acc[:],
+                    out=acc[:, cols],
                     lhsT=codes[:, 2 * g + half, :].bitcast(FP8X4),
                     lhsT_scale=scl[:, 2 * g + half, :],
-                    rhs=x_codes[:, g, :].bitcast(FP8X4),
-                    rhs_scale=x_scl[:, g, :],
+                    rhs=x_codes[:, g, cols].bitcast(FP8X4),
+                    rhs_scale=x_scl[:, g, cols],
                     start=(g == 0),
                     stop=(g == PASSES - 1),
                 )
-            by_chan = chan.tile([P, TOK], F32, name="by_chan")
             col = half * NH + h
-            nc.scalar.activation(out=by_chan[:], in_=acc[:], func=ACT.Identity, bias=bias_col[:, col:col + 1], scale=1.0)
-            chan_sb[(h, half)] = by_chan
+            nc.scalar.activation(out=by_chan[:, cols], in_=acc[:, cols], func=ACT.Identity, bias=bias_col[:, col:col + 1], scale=1.0)
 
-        def turn_back(h, half):
-            bt = bts.tile([P, B, HD], F32, name="bt")
-            for b in range(B):
-                nc.tensor.transpose(out=bt[:, b, :], in_=chan_sb[(h, half)][:, b * P:(b + 1) * P], identity=ident[:])
-            back_sb[(h, half)] = bt
+        def turn_back(h, half, first=0, last=B):
+            if first == 0:
+                bt = bts.tile([P, B, HD], F32, name="bt")
+                back_sb[(h, half)] = bt
+            for b in range(first, last):
+                nc.tensor.transpose(out=back_sb[(h, half)][:, b, :], in_=chan_sb[(h, half)][1][:, b * P:(b + 1) * P], identity=ident[:])
 
         def rotary_products(h):
             bt = back_sb[(h, 0)][:].rearrange("p b c -> p (b c)").unsqueeze(1).to_broadcast([P, 2, TOK])
@@ -256,14 +265,14 @@ def tile_gptneoxattention_pa_kernel(tc, x, wq_bytes, wq_scale, bq, wk, bk, out_0
                 op=ALU.add,
             )
 
-        def finish(h):
+        def finish(h, first=0, last=B):
             res = res_sb[h]
             nc.scalar.copy(
-                out=res[:, :, :, ROT:HD].rearrange("p b k r -> p (b k) r"),
-                in_=back_sb[(h, 1)][:].rearrange("p b (k r) -> p (b k) r", k=2),
+                out=res[:, first:last, :, ROT:HD].rearrange("p b k r -> p (b k) r"),
+                in_=back_sb[(h, 1)][:, first:last, :].rearrange("p b (k r) -> p (b k) r", k=2),
             )
-            nc.sync.dma_start(out=out_0[:, h, :, :].rearrange("b s d -> s b d"), in_=res[:, :, 0, :])
-            nc.sync.dma_start(out=out_1[:, h, :, :].rearrange("b s d -> s b d"), in_=res[:, :, 1, :])
+            nc.sync.dma_start(out=out_0[first:last, h, :, :].rearrange("b s d -> s b d"), in_=res[:, first:last, 0, :])
+            nc.sync.dma_start(out=out_1[first:last, h, :, :].rearrange("b s d -> s b d"), in_=res[:, first:last, 1, :])
 
         bias_f = const.tile([P, P], F32)
         nc.vector.tensor_copy(out=bias_f[:], in_=bias_rows[:])
@@ -280,6 +289,7 @@ def tile_gptneoxattention_pa_kernel(tc, x, wq_bytes, wq_scale, bq, wk, bk, out_0
         for b in range(B):
             turn_x(x_raw[b], xg_w, b)
         widen(1, 0, 1)
+        widen(2, 0, 2)
         for g in range(PASSES):
             nc.vector.quantize_mx(
                 out=x_codes[:, g, :].bitcast(FP8X4),
@@ -289,14 +299,17 @@ def tile_gptneoxattention_pa_kernel(tc, x, wq_bytes, wq_scale, bq, wk, bk, out_0
         turn(0, 0)
         turn(0, 1)
         quantize(0)
-        widen(2, 0, 1)
+        widen(2, 1, 2)
         turn(1, 1)
         turn(1, 0)
         quantize(1)
-        for n in range(2 * B):
-            nc.scalar.activation(out=table[:, :, n, :], in_=red4[:].rearrange("p (c r) -> p c r", c=2), func=ACT.Sin)
+        nc.scalar.activation(
+            out=table[:],
+            in_=red4[:].rearrange("p (c r) -> p c r", c=2).unsqueeze(2).to_broadcast([P, 2, 2 * B, ROT]),
+            func=ACT.Sin,
+        )
 
-        for j in range(NH + 1):
+        for j in range(NH):
             if j + AHEAD < NH:
                 load_q(j + AHEAD)
                 load_k(j + AHEAD)
@@ -309,8 +322,7 @@ def tile_gptneoxattention_pa_kernel(tc, x, wq_bytes, wq_scale, bq, wk, bk, out_0
             if j >= 1:
                 turn_back(j - 1, 0)
                 rotary_products(j - 1)
-            if j < NH:
-                multiply(j, 0)
+            multiply(j, 0)
             if j + 3 < NH:
                 widen(j + 3, 0, 1)
             if j >= 1:
@@ -321,5 +333,16 @@ def tile_gptneoxattention_pa_kernel(tc, x, wq_bytes, wq_scale, bq, wk, bk, out_0
             if j >= 1:
                 turn_back(j - 1, 1)
                 finish(j - 1)
-            if j < NH:
+            if j < NH - 1:
                 multiply(j, 1)
+
+        last = NH - 1
+        multiply(last, 1, 0, 2)
+        turn_back(last, 0)
+        rotary_products(last)
+        multiply(last, 1, 2, 4)
+        rotary_add(last)
+        turn_back(last, 1, 0, 2)
+        finish(last, 0, 2)
+        turn_back(last, 1, 2, 4)
+        finish(last, 2, 4)

@@ -21,7 +21,6 @@ TOK = SEQ * B
 ROT = 2 * RD
 FLOPS = 2 * SEQ * B * HID * 2 * NH * HD
 AHEAD = 6
-SORT_FROM = 3
 
 
 def tile_gptneoxattention_pa_kernel(tc, x, wq_bytes, wq_scale, bq, wk, bk, out_0, out_1):
@@ -32,8 +31,6 @@ def tile_gptneoxattention_pa_kernel(tc, x, wq_bytes, wq_scale, bq, wk, bk, out_0
         rows = ctx.enter_context(tc.tile_pool(name="rows", bufs=12))
         qbytes = ctx.enter_context(tc.tile_pool(name="qbytes", bufs=8))
         wide = ctx.enter_context(tc.tile_pool(name="wide", bufs=3))
-        sorted_k = ctx.enter_context(tc.tile_pool(name="sorted_k", bufs=3))
-        sorted_q = ctx.enter_context(tc.tile_pool(name="sorted_q", bufs=2))
         grouped = ctx.enter_context(tc.tile_pool(name="grouped", bufs=3))
         quant = ctx.enter_context(tc.tile_pool(name="quant", bufs=4))
         chan = ctx.enter_context(tc.tile_pool(name="chan", bufs=4))
@@ -146,8 +143,6 @@ def tile_gptneoxattention_pa_kernel(tc, x, wq_bytes, wq_scale, bq, wk, bk, out_0
         chan_sb = {}
         back_sb = {}
         res_sb = {}
-        sort_sb = {}
-        sort_q_sb = {}
         part_sb = {}
 
         def widen(h, part, parts):
@@ -157,22 +152,6 @@ def tile_gptneoxattention_pa_kernel(tc, x, wq_bytes, wq_scale, bq, wk, bk, out_0
             w = HID // parts
             cols = slice(part * w, (part + 1) * w)
             nc.vector.tensor_tensor(out=wide_sb[h][:, cols], in0=raw_q[h][:, cols].bitcast(FP8), in1=scale_bc[:, cols], op=ALU.mult)
-
-        def sort_words(h):
-            wk_sorted = sorted_k.tile([P, HID // 2], BF16, name="wk_sorted")
-            sort_sb[h] = wk_sorted
-            nc.scalar.copy(
-                out=wk_sorted[:].bitcast(F32).rearrange("p (g u c) -> p g u c", g=PASSES // 2, u=2),
-                in_=raw_k[h][:, 0:HID // 2].bitcast(F32).rearrange("p (g c u) -> p g u c", g=PASSES // 2, u=2),
-            )
-
-        def sort_last_pass(h):
-            wq_sorted = sorted_q.tile([P, 512], BF16, name="wq_sorted")
-            sort_q_sb[h] = wq_sorted
-            nc.scalar.copy(
-                out=wq_sorted[:].bitcast(F32).rearrange("p (u c) -> p u c", u=2),
-                in_=wide_sb[h][:, HID - 512:HID].bitcast(F32).rearrange("p (c u) -> p u c", u=2),
-            )
 
         def turn_x(src, grp_w, slot):
             words = src[:].bitcast(F32)
@@ -196,13 +175,7 @@ def tile_gptneoxattention_pa_kernel(tc, x, wq_bytes, wq_scale, bq, wk, bk, out_0
                 for g2 in range(2):
                     g = 2 * a + g2
                     for u in range(2):
-                        if kind == 1 and a == 0 and h in sort_sb:
-                            first = 256 * g + P * u
-                            nc.tensor.transpose(out=tp[:, u, g2, :], in_=sort_sb[h][:].bitcast(F32)[:, first:first + P], identity=ident[:])
-                        elif kind == 0 and g == PASSES - 1 and h in sort_q_sb:
-                            nc.tensor.transpose(out=tp[:, u, g2, :], in_=sort_q_sb[h][:].bitcast(F32)[:, P * u:P * (u + 1)], identity=ident[:])
-                        else:
-                            nc.tensor.transpose(out=tp[:, u, g2, :], in_=words[:, 256 * g + u:256 * (g + 1):2], identity=ident[:])
+                        nc.tensor.transpose(out=tp[:, u, g2, :], in_=words[:, 256 * g + u:256 * (g + 1):2], identity=ident[:])
                 nc.scalar.copy(
                     out=grp_w[:, 4 * a:4 * a + 4, kind * ROT:(kind + 1) * ROT, :],
                     in_=tp[:].rearrange("p u g (x r) -> p (g x) r u", x=2),
@@ -315,10 +288,6 @@ def tile_gptneoxattention_pa_kernel(tc, x, wq_bytes, wq_scale, bq, wk, bk, out_0
                 load_k(j + AHEAD)
             if j + 2 < NH:
                 turn(j + 2, 1)
-            if SORT_FROM <= j + 2 < NH:
-                sort_last_pass(j + 2)
-            if SORT_FROM <= j + 3 < NH:
-                sort_words(j + 3)
             if j >= 1:
                 turn_back(j - 1, 0)
                 rotary_products(j - 1)

@@ -34,12 +34,14 @@ def tile_gptneoxattention_pa_kernel(tc, x, wq_bytes, wq_scale, bq, wk, bk, out_0
         grouped = ctx.enter_context(tc.tile_pool(name="grouped", bufs=3))
         quant = ctx.enter_context(tc.tile_pool(name="quant", bufs=4))
         chan = ctx.enter_context(tc.tile_pool(name="chan", bufs=4))
-        outp = ctx.enter_context(tc.tile_pool(name="outp", bufs=3))
-        tmp = ctx.enter_context(tc.tile_pool(name="tmp", bufs=2))
+        outp = ctx.enter_context(tc.tile_pool(name="outp", bufs=4))
+        tmp = ctx.enter_context(tc.tile_pool(name="tmp", bufs=3))
         tps = ctx.enter_context(tc.psum_pool(name="tps", bufs=4))
         accs = ctx.enter_context(tc.psum_pool(name="accs", bufs=2))
         bts = ctx.enter_context(tc.psum_pool(name="bts", bufs=2))
 
+        scale_rows = const.tile([P, P], F32)
+        nc.gpsimd.memset(scale_rows[:], 0.0)
         warm = const.tile([P, 8], F32)
         nc.vector.memset(warm[:], 0.0)
         nc.scalar.activation(out=warm[:], in_=warm[:], func=ACT.Sin)
@@ -47,8 +49,6 @@ def tile_gptneoxattention_pa_kernel(tc, x, wq_bytes, wq_scale, bq, wk, bk, out_0
         masks.make_identity(nc, ident[:])
         bias_rows = const.tile([P, P], BF16)
         nc.vector.memset(bias_rows[:], 0.0)
-        scale_rows = const.tile([P, P], F32)
-        nc.vector.memset(scale_rows[:], 0.0)
 
         scale_bc = const.tile([P, HID], F32)
         raw_q = {}
@@ -89,18 +89,6 @@ def tile_gptneoxattention_pa_kernel(tc, x, wq_bytes, wq_scale, bq, wk, bk, out_0
             load_q(h)
             load_k(h)
 
-        sc_ps = tps.tile([P, 2, 2, P], F32, name="tp")
-        nc.tensor.transpose(out=sc_ps[:, 0, 0, :], in_=scale_rows[:], identity=ident[:])
-        scale_col = const.tile([P, HID // P], F32)
-        nc.scalar.copy(out=scale_col[:], in_=sc_ps[:, 0, 0, 0:HID // P])
-        for q in range(4):
-            bc_ps = tps.tile([P, 2, 2, P], F32, name="tp")
-            for a in range(2):
-                for u in range(2):
-                    c = 4 * q + 2 * a + u
-                    nc.tensor.transpose(out=bc_ps[:, a, u, :], in_=scale_col[:, c:c + 1].to_broadcast([P, P]), identity=ident[:])
-            nc.scalar.copy(out=scale_bc[:, q * 512:(q + 1) * 512], in_=bc_ps[:].rearrange("p a u r -> p (a u r)"))
-
         pos = const.tile([P, ROT], F32)
         nc.gpsimd.iota(out=pos[:], pattern=[[0, ROT]], base=0, channel_multiplier=1, allow_small_or_imprecise_dtypes=True)
         sign = const.tile([P, ROT], F32)
@@ -119,23 +107,24 @@ def tile_gptneoxattention_pa_kernel(tc, x, wq_bytes, wq_scale, bq, wk, bk, out_0
         nc.vector.tensor_copy(out=turns_i[:], in_=turns[:])
         turns_f = const.tile([P, 2 * ROT], F32)
         nc.vector.tensor_copy(out=turns_f[:], in_=turns_i[:])
-        two_pi_hi = 6.28125
-        two_pi_lo = 2.0 * math.pi - two_pi_hi
-        red1 = const.tile([P, 2 * ROT], F32)
-        nc.vector.scalar_tensor_tensor(out=red1[:], in0=turns_f[:], scalar=-two_pi_hi, in1=arg[:], op0=ALU.mult, op1=ALU.add)
-        red2 = const.tile([P, 2 * ROT], F32)
-        nc.vector.scalar_tensor_tensor(out=red2[:], in0=turns_f[:], scalar=-two_pi_lo, in1=red1[:], op0=ALU.mult, op1=ALU.add)
-        over = const.tile([P, 2 * ROT], F32)
-        nc.vector.tensor_single_scalar(out=over[:], in_=red2[:], scalar=math.pi, op=ALU.is_gt)
-        red3 = const.tile([P, 2 * ROT], F32)
-        nc.vector.scalar_tensor_tensor(out=red3[:], in0=over[:], scalar=-2.0 * math.pi, in1=red2[:], op0=ALU.mult, op1=ALU.add)
-        under = const.tile([P, 2 * ROT], F32)
-        nc.vector.tensor_single_scalar(out=under[:], in_=red3[:], scalar=-math.pi, op=ALU.is_lt)
-        red4 = const.tile([P, 2 * ROT], F32)
-        nc.vector.scalar_tensor_tensor(out=red4[:], in0=under[:], scalar=2.0 * math.pi, in1=red3[:], op0=ALU.mult, op1=ALU.add)
+        red = const.tile([P, 2 * ROT], F32)
+        nc.vector.scalar_tensor_tensor(out=red[:], in0=turns_f[:], scalar=-2.0 * math.pi, in1=arg[:], op0=ALU.mult, op1=ALU.add)
         table = const.tile([P, 2, 2 * B, ROT], F32)
         cos_t = table[:, 0, :, :]
         sin_t = table[:, 1, :, :]
+
+        sc_ps = tps.tile([P, 2, 2, P], F32, name="tp")
+        nc.tensor.transpose(out=sc_ps[:, 0, 0, :], in_=scale_rows[:], identity=ident[:])
+        scale_col = const.tile([P, HID // P], F32)
+        nc.scalar.copy(out=scale_col[:], in_=sc_ps[:, 0, 0, 0:HID // P])
+        for q in range(4):
+            bc_ps = tps.tile([P, 2, 2, P], F32, name="tp")
+            for a in range(2):
+                for u in range(2):
+                    c = 4 * q + 2 * a + u
+                    nc.tensor.transpose(out=bc_ps[:, a, u, :], in_=scale_col[:, c:c + 1].to_broadcast([P, P]), identity=ident[:])
+            spread = nc.vector.tensor_copy if q == 0 else nc.scalar.copy
+            spread(out=scale_bc[:, q * 512:(q + 1) * 512], in_=bc_ps[:].rearrange("p a u r -> p (a u r)"))
 
         wide_sb = {}
         grp_sb = {}
@@ -227,16 +216,22 @@ def tile_gptneoxattention_pa_kernel(tc, x, wq_bytes, wq_scale, bq, wk, bk, out_0
                 out=parts[:].rearrange("p c n r -> p c (n r)"), in0=bt, in1=table[:].rearrange("p c n r -> p c (n r)"), op=ALU.mult
             )
 
-        def rotary_add(h):
+        def rotary_add(h, kind, engine):
+            if h not in res_sb:
+                res = outp.tile([P, B, 2, HD], F32, name="res")
+                res_sb[h] = res
             part_c, part_s = part_sb[h]
-            res = outp.tile([P, B, 2, HD], F32, name="res")
-            res_sb[h] = res
-            nc.vector.tensor_tensor(
-                out=res[:, :, :, 0:ROT].rearrange("p b k (j e) -> p (b k) j e", e=2),
-                in0=part_c.rearrange("p n (j e) -> p n j e", e=2),
-                in1=part_s.rearrange("p n (j e) -> p n j e", e=2)[:, :, :, ::-1],
+            engine.tensor_tensor(
+                out=res_sb[h][:, :, kind, 0:ROT].rearrange("p b (j e) -> p b j e", e=2),
+                in0=part_c[:, kind::2, :].rearrange("p b (j e) -> p b j e", e=2),
+                in1=part_s[:, kind::2, :].rearrange("p b (j e) -> p b j e", e=2)[:, :, :, ::-1],
                 op=ALU.add,
             )
+
+        def add_on_gpsimd(h, after):
+            mark = tmp.tile([P, 1], U32, name="mark")
+            nc.gpsimd.tensor_copy(out=mark[:], in_=code_sb[after][0][:, 0, 0:1])
+            rotary_add(h, 1, nc.gpsimd)
 
         def finish(h, first=0, last=B):
             res = res_sb[h]
@@ -244,8 +239,10 @@ def tile_gptneoxattention_pa_kernel(tc, x, wq_bytes, wq_scale, bq, wk, bk, out_0
                 out=res[:, first:last, :, ROT:HD].rearrange("p b k r -> p (b k) r"),
                 in_=back_sb[(h, 1)][:, first:last, :].rearrange("p b (k r) -> p (b k) r", k=2),
             )
-            nc.sync.dma_start(out=out_0[first:last, h, :, :].rearrange("b s d -> s b d"), in_=res[:, first:last, 0, :])
-            nc.sync.dma_start(out=out_1[first:last, h, :, :].rearrange("b s d -> s b d"), in_=res[:, first:last, 1, :])
+
+        def store(h, first=0, last=B):
+            nc.sync.dma_start(out=out_0[first:last, h, :, :].rearrange("b s d -> s b d"), in_=res_sb[h][:, first:last, 0, :])
+            nc.sync.dma_start(out=out_1[first:last, h, :, :].rearrange("b s d -> s b d"), in_=res_sb[h][:, first:last, 1, :])
 
         bias_f = const.tile([P, P], F32)
         nc.vector.tensor_copy(out=bias_f[:], in_=bias_rows[:])
@@ -278,7 +275,7 @@ def tile_gptneoxattention_pa_kernel(tc, x, wq_bytes, wq_scale, bq, wk, bk, out_0
         quantize(1)
         nc.scalar.activation(
             out=table[:],
-            in_=red4[:].rearrange("p (c r) -> p c r", c=2).unsqueeze(2).to_broadcast([P, 2, 2 * B, ROT]),
+            in_=red[:].rearrange("p (c r) -> p c r", c=2).unsqueeze(2).to_broadcast([P, 2, 2 * B, ROT]),
             func=ACT.Sin,
         )
 
@@ -286,22 +283,31 @@ def tile_gptneoxattention_pa_kernel(tc, x, wq_bytes, wq_scale, bq, wk, bk, out_0
             if j + AHEAD < NH:
                 load_q(j + AHEAD)
                 load_k(j + AHEAD)
+            if j == 0:
+                multiply(0, 0)
             if j + 2 < NH:
                 turn(j + 2, 1)
             if j >= 1:
                 turn_back(j - 1, 0)
                 rotary_products(j - 1)
-            multiply(j, 0)
+                multiply(j, 0)
+            if 2 <= j < NH - 1:
+                add_on_gpsimd(j - 2, j + 1)
+                store(j - 2)
             if j + 3 < NH:
                 widen(j + 3, 0, 1)
             if j >= 1:
-                rotary_add(j - 1)
+                rotary_add(j - 1, 0, nc.vector)
+            if j >= NH - 2:
+                rotary_add(j - 1, 1, nc.vector)
             if j + 2 < NH:
                 turn(j + 2, 0)
                 quantize(j + 2)
             if j >= 1:
                 turn_back(j - 1, 1)
                 finish(j - 1)
+            if j >= NH - 2:
+                store(j - 1)
             if j < NH - 1:
                 multiply(j, 1)
 
@@ -310,8 +316,11 @@ def tile_gptneoxattention_pa_kernel(tc, x, wq_bytes, wq_scale, bq, wk, bk, out_0
         turn_back(last, 0)
         rotary_products(last)
         multiply(last, 1, 2, 4)
-        rotary_add(last)
+        rotary_add(last, 0, nc.vector)
+        rotary_add(last, 1, nc.vector)
         turn_back(last, 1, 0, 2)
         finish(last, 0, 2)
+        store(last, 0, 2)
         turn_back(last, 1, 2, 4)
         finish(last, 2, 4)
+        store(last, 2, 4)

@@ -34,8 +34,8 @@ def tile_gptneoxattention_pa_kernel(tc, x, wq_bytes, wq_scale, bq, wk, bk, out_0
         grouped = ctx.enter_context(tc.tile_pool(name="grouped", bufs=3))
         quant = ctx.enter_context(tc.tile_pool(name="quant", bufs=4))
         chan = ctx.enter_context(tc.tile_pool(name="chan", bufs=4))
-        outp = ctx.enter_context(tc.tile_pool(name="outp", bufs=4))
-        tmp = ctx.enter_context(tc.tile_pool(name="tmp", bufs=3))
+        outp = ctx.enter_context(tc.tile_pool(name="outp", bufs=5))
+        tmp = ctx.enter_context(tc.tile_pool(name="tmp", bufs=4))
         tps = ctx.enter_context(tc.psum_pool(name="tps", bufs=4))
         accs = ctx.enter_context(tc.psum_pool(name="accs", bufs=2))
         bts = ctx.enter_context(tc.psum_pool(name="bts", bufs=2))
@@ -92,7 +92,7 @@ def tile_gptneoxattention_pa_kernel(tc, x, wq_bytes, wq_scale, bq, wk, bk, out_0
         pos = const.tile([P, ROT], F32)
         nc.gpsimd.iota(out=pos[:], pattern=[[0, ROT]], base=0, channel_multiplier=1, allow_small_or_imprecise_dtypes=True)
         sign = const.tile([P, ROT], F32)
-        nc.gpsimd.iota(out=sign[:], pattern=[[0, RD], [-2, 2]], base=1, channel_multiplier=0, allow_small_or_imprecise_dtypes=True)
+        nc.gpsimd.iota(out=sign[:], pattern=[[0, RD], [2, 2]], base=-1, channel_multiplier=0, allow_small_or_imprecise_dtypes=True)
         ang = const.tile([P, ROT], F32)
         ang_v = ang[:].rearrange("p (a f e) -> p a f e", a=2, e=2)
         pos_v = pos[:].rearrange("p (a f e) -> p a f e", a=2, e=2)
@@ -109,9 +109,9 @@ def tile_gptneoxattention_pa_kernel(tc, x, wq_bytes, wq_scale, bq, wk, bk, out_0
         nc.vector.tensor_copy(out=turns_f[:], in_=turns_i[:])
         red = const.tile([P, 2 * ROT], F32)
         nc.vector.scalar_tensor_tensor(out=red[:], in0=turns_f[:], scalar=-2.0 * math.pi, in1=arg[:], op0=ALU.mult, op1=ALU.add)
-        table = const.tile([P, 2, 2 * B, ROT], F32)
-        cos_t = table[:, 0, :, :]
-        sin_t = table[:, 1, :, :]
+        table = const.tile([P, 2, 2, ROT], F32)
+        ident_b = const.tile([P, P], BF16)
+        nc.vector.tensor_copy(out=ident_b[:], in_=ident[:])
 
         sc_ps = tps.tile([P, 2, 2, P], F32, name="tp")
         nc.tensor.transpose(out=sc_ps[:, 0, 0, :], in_=scale_rows[:], identity=ident[:])
@@ -129,10 +129,12 @@ def tile_gptneoxattention_pa_kernel(tc, x, wq_bytes, wq_scale, bq, wk, bk, out_0
         wide_sb = {}
         grp_sb = {}
         code_sb = {}
+        acc_ps = {}
         chan_sb = {}
         back_sb = {}
+        cos_sb = {}
+        sin_sb = {}
         res_sb = {}
-        part_sb = {}
 
         def widen(h, part, parts):
             if part == 0:
@@ -180,69 +182,122 @@ def tile_gptneoxattention_pa_kernel(tc, x, wq_bytes, wq_scale, bq, wk, bk, out_0
             )
             code_sb[h] = (codes, scl)
 
-        def multiply(h, half, first=0, last=B):
+        def multiply_rot(h):
             codes, scl = code_sb[h]
-            if first == 0:
-                acc = accs.tile([P, TOK], F32, name="acc")
-                by_chan = chan.tile([P, TOK], F32, name="by_chan")
-                chan_sb[(h, half)] = (acc, by_chan)
-            acc, by_chan = chan_sb[(h, half)]
-            cols = slice(first * P, last * P)
+            acc = accs.tile([P, TOK], F32, name="acc")
+            acc_ps[(h, 0)] = acc
             for g in range(PASSES):
                 nc.tensor.matmul_mx(
-                    out=acc[:, cols],
-                    lhsT=codes[:, 2 * g + half, :].bitcast(FP8X4),
-                    lhsT_scale=scl[:, 2 * g + half, :],
-                    rhs=x_codes[:, g, cols].bitcast(FP8X4),
-                    rhs_scale=x_scl[:, g, cols],
+                    out=acc[:],
+                    lhsT=codes[:, 2 * g, :].bitcast(FP8X4),
+                    lhsT_scale=scl[:, 2 * g, :],
+                    rhs=x_codes[:, g, :].bitcast(FP8X4),
+                    rhs_scale=x_scl[:, g, :],
                     start=(g == 0),
                     stop=(g == PASSES - 1),
                 )
-            col = half * NH + h
-            nc.scalar.activation(out=by_chan[:, cols], in_=acc[:, cols], func=ACT.Identity, bias=bias_col[:, col:col + 1], scale=1.0)
 
-        def turn_back(h, half, first=0, last=B):
+        def add_rot_bias(h):
+            by_chan = chan.tile([P, TOK], F32, name="by_chan")
+            chan_sb[h] = by_chan
+            nc.scalar.activation(out=by_chan[:], in_=acc_ps[(h, 0)][:], func=ACT.Identity, bias=bias_col[:, h:h + 1], scale=1.0)
+
+        def multiply_pass(h, first=0, last=B):
+            codes, scl = code_sb[h]
             if first == 0:
-                bt = bts.tile([P, B, HD], F32, name="bt")
-                back_sb[(h, half)] = bt
+                acc = accs.tile([P, TOK], F32, name="acc")
+                acc_ps[(h, 1)] = acc
             for b in range(first, last):
-                nc.tensor.transpose(out=back_sb[(h, half)][:, b, :], in_=chan_sb[(h, half)][1][:, b * P:(b + 1) * P], identity=ident[:])
+                cols = slice(b * P, (b + 1) * P)
+                for g in range(PASSES):
+                    nc.tensor.matmul_mx(
+                        out=acc_ps[(h, 1)][:, cols],
+                        lhsT=x_codes[:, g, cols].bitcast(FP8X4),
+                        lhsT_scale=x_scl[:, g, cols],
+                        rhs=codes[:, 2 * g + 1, :].bitcast(FP8X4),
+                        rhs_scale=scl[:, 2 * g + 1, :],
+                        start=(g == 0),
+                        stop=(g == PASSES - 1),
+                    )
 
-        def rotary_products(h):
-            bt = back_sb[(h, 0)][:].rearrange("p b c -> p (b c)").unsqueeze(1).to_broadcast([P, 2, TOK])
-            parts = tmp.tile([P, 2, 2 * B, ROT], F32, name="parts")
-            part_sb[h] = (parts[:, 0, :, :], parts[:, 1, :, :])
+        def add_bias(h):
+            res = outp.tile([P, B, 2, HD], F32, name="res")
+            res_sb[h] = res
             nc.vector.tensor_tensor(
-                out=parts[:].rearrange("p c n r -> p c (n r)"), in0=bt, in1=table[:].rearrange("p c n r -> p c (n r)"), op=ALU.mult
+                out=res[:, :, :, ROT:HD],
+                in0=acc_ps[(h, 1)][:].rearrange("p (b k r) -> p b k r", b=B, k=2),
+                in1=bias_bc[:, h, :, :].unsqueeze(1).to_broadcast([P, B, 2, ROT]),
+                op=ALU.add,
             )
 
-        def rotary_add(h, kind, engine):
-            if h not in res_sb:
-                res = outp.tile([P, B, 2, HD], F32, name="res")
-                res_sb[h] = res
-            part_c, part_s = part_sb[h]
+        def turn_back(h):
+            bt = bts.tile([P, B, HD], F32, name="bt")
+            back_sb[h] = bt
+            for b in range(B):
+                nc.tensor.transpose(out=bt[:, b, :], in_=chan_sb[h][:, b * P:(b + 1) * P], identity=ident[:])
+
+        def cosine_products(h, first, last):
+            if first == 0:
+                part_c = tmp.tile([P, 2 * B, ROT], F32, name="part_c")
+                cos_sb[h] = part_c
+            t_v = back_sb[h][:].rearrange("p b (k a f e) -> p (b k a) f e", k=2, a=2, e=2)
+            out_v = cos_sb[h][:].rearrange("p n (a f e) -> p (n a) f e", a=2, e=2)
+            for f in range(first, last):
+                nc.scalar.activation(out=out_v[:, :, f, :], in_=t_v[:, :, f, :], func=ACT.Copy, scale=table[:, 0, 0, 2 * f:2 * f + 1])
+
+        def cosine_on_vector(h):
+            part_c = tmp.tile([P, 2 * B, ROT], F32, name="part_c")
+            cos_sb[h] = part_c
+            nc.vector.tensor_tensor(
+                out=part_c[:].rearrange("p (b k) r -> p b (k r)", b=B),
+                in0=back_sb[h][:],
+                in1=table[:, 0, :, :].rearrange("p k r -> p (k r)").unsqueeze(1).to_broadcast([P, B, 2 * ROT]),
+                op=ALU.mult,
+            )
+
+        def sine_products(h):
+            part_s = tmp.tile([P, 2 * B, ROT], F32, name="part_s")
+            sin_sb[h] = part_s
+            nc.vector.tensor_tensor(
+                out=part_s[:].rearrange("p (b k) (j e) -> p b (k j) e", b=B, e=2),
+                in0=back_sb[h][:].rearrange("p b (i e) -> p b i e", e=2)[:, :, :, ::-1],
+                in1=table[:, 1, :, :].rearrange("p k (j e) -> p (k j) e", e=2).unsqueeze(1).to_broadcast([P, B, 2 * RD, 2]),
+                op=ALU.mult,
+            )
+
+        def rotary_add(h, first, last, engine):
             engine.tensor_tensor(
-                out=res_sb[h][:, :, kind, 0:ROT].rearrange("p b (j e) -> p b j e", e=2),
-                in0=part_c[:, kind::2, :].rearrange("p b (j e) -> p b j e", e=2),
-                in1=part_s[:, kind::2, :].rearrange("p b (j e) -> p b j e", e=2)[:, :, :, ::-1],
+                out=res_sb[h][:, :, first:last, 0:ROT],
+                in0=cos_sb[h][:].rearrange("p (b k) r -> p b k r", b=B)[:, :, first:last, :],
+                in1=sin_sb[h][:].rearrange("p (b k) r -> p b k r", b=B)[:, :, first:last, :],
                 op=ALU.add,
             )
 
         def add_on_gpsimd(h, after):
             mark = tmp.tile([P, 1], U32, name="mark")
             nc.gpsimd.tensor_copy(out=mark[:], in_=code_sb[after][0][:, 0, 0:1])
-            rotary_add(h, 1, nc.gpsimd)
+            rotary_add(h, 1, 2, nc.gpsimd)
 
-        def finish(h, first=0, last=B):
-            res = res_sb[h]
+        def store(h):
+            nc.sync.dma_start(out=out_0[:, h, :, :].rearrange("b s d -> s b d"), in_=res_sb[h][:, :, 0, :])
+            nc.sync.dma_start(out=out_1[:, h, :, :].rearrange("b s d -> s b d"), in_=res_sb[h][:, :, 1, :])
+
+        bias_bc = const.tile([P, NH, 2, ROT], BF16)
+
+        spread_ps = {}
+
+        def spread_bias(half):
+            bias_ps = tps.tile([P, 8, P], BF16, name="tp")
+            spread_ps[half] = bias_ps
+            for i in range(8):
+                row = NH + 8 * half + i
+                nc.tensor.matmul(out=bias_ps[:, i, :], lhsT=ident_b[:, row:row + 1].to_broadcast([P, P]), rhs=bias_rows[:], start=True, stop=True)
+
+        def copy_bias(half):
             nc.scalar.copy(
-                out=res[:, first:last, :, ROT:HD].rearrange("p b k r -> p (b k) r"),
-                in_=back_sb[(h, 1)][:, first:last, :].rearrange("p b (k r) -> p (b k) r", k=2),
+                out=bias_bc[:, 8 * half:8 * half + 8, :, :].rearrange("p h k r -> p (h k r)"),
+                in_=spread_ps[half][:].rearrange("p h c -> p (h c)"),
             )
-
-        def store(h, first=0, last=B):
-            nc.sync.dma_start(out=out_0[first:last, h, :, :].rearrange("b s d -> s b d"), in_=res_sb[h][:, first:last, 0, :])
-            nc.sync.dma_start(out=out_1[first:last, h, :, :].rearrange("b s d -> s b d"), in_=res_sb[h][:, first:last, 1, :])
 
         bias_f = const.tile([P, P], F32)
         nc.vector.tensor_copy(out=bias_f[:], in_=bias_rows[:])
@@ -256,8 +311,10 @@ def tile_gptneoxattention_pa_kernel(tc, x, wq_bytes, wq_scale, bq, wk, bk, out_0
         xg_w = xg[:].bitcast(F32).rearrange("p (g c u) -> p g c u", g=PASSES, u=2)
         x_codes = const.tile([P, PASSES, TOK], U32, align_bytes=64)
         x_scl = const.tile([P, PASSES, TOK], U8, align_bytes=64)
-        for b in range(B):
-            turn_x(x_raw[b], xg_w, b)
+        turn_x(x_raw[0], xg_w, 0)
+        turn_x(x_raw[1], xg_w, 1)
+        turn_x(x_raw[2], xg_w, 2)
+        turn_x(x_raw[3], xg_w, 3)
         widen(1, 0, 1)
         widen(2, 0, 2)
         for g in range(PASSES):
@@ -272,10 +329,11 @@ def tile_gptneoxattention_pa_kernel(tc, x, wq_bytes, wq_scale, bq, wk, bk, out_0
         widen(2, 1, 2)
         turn(1, 1)
         turn(1, 0)
+        spread_bias(0)
         quantize(1)
         nc.scalar.activation(
             out=table[:],
-            in_=red[:].rearrange("p (c r) -> p c r", c=2).unsqueeze(2).to_broadcast([P, 2, 2 * B, ROT]),
+            in_=red[:].rearrange("p (c r) -> p c r", c=2).unsqueeze(2).to_broadcast([P, 2, 2, ROT]),
             func=ACT.Sin,
         )
 
@@ -284,43 +342,53 @@ def tile_gptneoxattention_pa_kernel(tc, x, wq_bytes, wq_scale, bq, wk, bk, out_0
                 load_q(j + AHEAD)
                 load_k(j + AHEAD)
             if j == 0:
-                multiply(0, 0)
+                multiply_rot(0)
             if j + 2 < NH:
                 turn(j + 2, 1)
             if j >= 1:
-                turn_back(j - 1, 0)
-                rotary_products(j - 1)
-                multiply(j, 0)
-            if 2 <= j < NH - 1:
-                add_on_gpsimd(j - 2, j + 1)
-                store(j - 2)
+                add_bias(j - 1)
+                turn_back(j - 1)
+                if j < NH - 1:
+                    cosine_products(j - 1, 0, 8)
+            if j >= 2:
+                sine_products(j - 2)
+            if 3 <= j < NH - 1:
+                add_on_gpsimd(j - 3, j + 1)
+                store(j - 3)
+            if j >= 1:
+                multiply_rot(j)
+            add_rot_bias(j)
             if j + 3 < NH:
                 widen(j + 3, 0, 1)
-            if j >= 1:
-                rotary_add(j - 1, 0, nc.vector)
-            if j >= NH - 2:
-                rotary_add(j - 1, 1, nc.vector)
+            if j >= 2:
+                rotary_add(j - 2, 0, 1, nc.vector)
             if j + 2 < NH:
                 turn(j + 2, 0)
                 quantize(j + 2)
-            if j >= 1:
-                turn_back(j - 1, 1)
-                finish(j - 1)
-            if j >= NH - 2:
-                store(j - 1)
+            if 1 <= j < NH - 1:
+                cosine_products(j - 1, 8, RD // 2)
+            if j == 0:
+                copy_bias(0)
+            if j == 4:
+                spread_bias(1)
+                copy_bias(1)
             if j < NH - 1:
-                multiply(j, 1)
+                multiply_pass(j)
 
         last = NH - 1
-        multiply(last, 1, 0, 2)
-        turn_back(last, 0)
-        rotary_products(last)
-        multiply(last, 1, 2, 4)
-        rotary_add(last, 0, nc.vector)
-        rotary_add(last, 1, nc.vector)
-        turn_back(last, 1, 0, 2)
-        finish(last, 0, 2)
-        store(last, 0, 2)
-        turn_back(last, 1, 2, 4)
-        finish(last, 2, 4)
-        store(last, 2, 4)
+        multiply_pass(last, 0, 2)
+        turn_back(last)
+        rotary_add(last - 3, 1, 2, nc.gpsimd)
+        store(last - 3)
+        rotary_add(last - 2, 1, 2, nc.gpsimd)
+        store(last - 2)
+        cosine_on_vector(last - 1)
+        sine_products(last - 1)
+        rotary_add(last - 1, 0, 2, nc.vector)
+        store(last - 1)
+        cosine_on_vector(last)
+        sine_products(last)
+        multiply_pass(last, 2, 4)
+        add_bias(last)
+        rotary_add(last, 0, 2, nc.vector)
+        store(last)

from contextlib import ExitStack
import math

import concourse.masks as masks
import concourse.mybir as mybir

F32 = mybir.dt.float32
BF16 = mybir.dt.bfloat16
U32 = mybir.dt.uint32
U8 = mybir.dt.uint8
I32 = mybir.dt.int32
FP8 = mybir.dt.float8_e4m3fn
FP8X4 = mybir.dt.float8_e4m3fn_x4
ALU = mybir.AluOpType
ACT = mybir.ActivationFunctionType

SEQ, B, HID, NH, HD, RD = 128, 4, 2048, 16, 128, 32
P = 128
PASSES = HID // 512
TOK = SEQ * B
ROT = 2 * RD
FLOPS = 2 * SEQ * B * HID * 2 * NH * HD
AHEAD = 6


def tile_gptneoxattention_pa_kernel(tc, x, wq_bytes, wq_scale, bq, wk, bk, out_0, out_1):
    nc = tc.nc
    with ExitStack() as ctx:
        ctx.enter_context(tc.manual_schedule())
        const = ctx.enter_context(tc.tile_pool(name="const", bufs=1))
        rows = ctx.enter_context(tc.tile_pool(name="rows", bufs=12))
        qbytes = ctx.enter_context(tc.tile_pool(name="qbytes", bufs=8))
        wide = ctx.enter_context(tc.tile_pool(name="wide", bufs=3))
        grouped = ctx.enter_context(tc.tile_pool(name="grouped", bufs=3))
        quant = ctx.enter_context(tc.tile_pool(name="quant", bufs=4))
        chan = ctx.enter_context(tc.tile_pool(name="chan", bufs=4))
        outp = ctx.enter_context(tc.tile_pool(name="outp", bufs=5))
        tmp = ctx.enter_context(tc.tile_pool(name="tmp", bufs=4))
        tps = ctx.enter_context(tc.psum_pool(name="tps", bufs=4))
        accs = ctx.enter_context(tc.psum_pool(name="accs", bufs=2))
        bts = ctx.enter_context(tc.psum_pool(name="bts", bufs=2))

        scale_rows = const.tile([P, P], F32)
        nc.gpsimd.memset(scale_rows[:], 0.0)
        warm = const.tile([P, 8], F32)
        nc.vector.memset(warm[:], 0.0)
        nc.scalar.activation(out=warm[:], in_=warm[:], func=ACT.Sin)
        ident = const.tile([P, P], F32)
        masks.make_identity(nc, ident[:])
        bias_rows = const.tile([P, P], BF16)
        nc.vector.memset(bias_rows[:], 0.0)

        scale_bc = const.tile([P, HID], F32)
        raw_q = {}
        raw_k = {}

        def load_q(h):
            wq_bytes_sb = qbytes.tile([P, HID], U8, name="wq_bytes_sb")
            nc.sync.dma_start(out=wq_bytes_sb[:], in_=wq_bytes[h * P:(h + 1) * P, :])
            raw_q[h] = wq_bytes_sb

        def load_k(h):
            row_sb = rows.tile([P, HID], BF16, name="row_sb")
            nc.sync.dma_start(out=row_sb[:], in_=wk[h * P:(h + 1) * P, :])
            raw_k[h] = row_sb

        x_raw = []

        def load_x(b):
            row_sb = rows.tile([P, HID], BF16, name="row_sb")
            nc.sync.dma_start(out=row_sb[:], in_=x[:, b, :])
            x_raw.append(row_sb)

        nc.sync.dma_start(out=scale_rows[0:HID // P, :], in_=wq_scale.rearrange("o (c j) -> (o c) j", j=P))
        for kind, vec in ((0, bq), (1, bk)):
            halves = vec.rearrange("(h x r) -> x h r", x=2, r=ROT)
            for half in range(2):
                nc.sync.dma_start(out=bias_rows[half * NH:(half + 1) * NH, kind * ROT:(kind + 1) * ROT], in_=halves[half])
        load_q(0)
        load_x(0)
        load_x(1)
        load_q(1)
        load_x(2)
        load_x(3)
        load_q(2)
        for h in range(3):
            load_k(h)
        for h in range(3, AHEAD):
            load_q(h)
            load_k(h)

        pos = const.tile([P, ROT], F32)
        nc.gpsimd.iota(out=pos[:], pattern=[[0, ROT]], base=0, channel_multiplier=1, allow_small_or_imprecise_dtypes=True)
        sign = const.tile([P, ROT], F32)
        nc.gpsimd.iota(out=sign[:], pattern=[[0, RD], [2, 2]], base=-1, channel_multiplier=0, allow_small_or_imprecise_dtypes=True)
        ang = const.tile([P, ROT], F32)
        ang_v = ang[:].rearrange("p (a f e) -> p a f e", a=2, e=2)
        pos_v = pos[:].rearrange("p (a f e) -> p a f e", a=2, e=2)
        for f in range(RD // 2):
            nc.vector.tensor_scalar_mul(out=ang_v[:, :, f, :], in0=pos_v[:, :, f, :], scalar1=1.0 / 10000.0 ** (2.0 * f / RD))
        arg = const.tile([P, 2 * ROT], F32)
        nc.vector.tensor_scalar_add(out=arg[:, 0:ROT], in0=ang[:], scalar1=math.pi / 2.0)
        nc.vector.tensor_tensor(out=arg[:, ROT:2 * ROT], in0=ang[:], in1=sign[:], op=ALU.mult)
        turns = const.tile([P, 2 * ROT], F32)
        nc.vector.tensor_scalar_mul(out=turns[:], in0=arg[:], scalar1=1.0 / (2.0 * math.pi))
        turns_i = const.tile([P, 2 * ROT], I32)
        nc.vector.tensor_copy(out=turns_i[:], in_=turns[:])
        turns_f = const.tile([P, 2 * ROT], F32)
        nc.vector.tensor_copy(out=turns_f[:], in_=turns_i[:])
        red = const.tile([P, 2 * ROT], F32)
        nc.vector.scalar_tensor_tensor(out=red[:], in0=turns_f[:], scalar=-2.0 * math.pi, in1=arg[:], op0=ALU.mult, op1=ALU.add)
        table = const.tile([P, 2, 2, ROT], F32)
        ident_b = const.tile([P, P], BF16)
        nc.vector.tensor_copy(out=ident_b[:], in_=ident[:])

        sc_ps = tps.tile([P, 2, 2, P], F32, name="tp")
        nc.tensor.transpose(out=sc_ps[:, 0, 0, :], in_=scale_rows[:], identity=ident[:])
        scale_col = const.tile([P, HID // P], F32)
        nc.scalar.copy(out=scale_col[:], in_=sc_ps[:, 0, 0, 0:HID // P])
        for q in range(4):
            bc_ps = tps.tile([P, 2, 2, P], F32, name="tp")
            for a in range(2):
                for u in range(2):
                    c = 4 * q + 2 * a + u
                    nc.tensor.transpose(out=bc_ps[:, a, u, :], in_=scale_col[:, c:c + 1].to_broadcast([P, P]), identity=ident[:])
            spread = nc.vector.tensor_copy if q == 0 else nc.scalar.copy
            spread(out=scale_bc[:, q * 512:(q + 1) * 512], in_=bc_ps[:].rearrange("p a u r -> p (a u r)"))

        wide_sb = {}
        grp_sb = {}
        code_sb = {}
        acc_ps = {}
        chan_sb = {}
        back_sb = {}
        cos_sb = {}
        sin_sb = {}
        res_sb = {}

        def widen(h, part, parts):
            if part == 0:
                wq_wide = wide.tile([P, HID], BF16, name="wq_wide")
                wide_sb[h] = wq_wide
            w = HID // parts
            cols = slice(part * w, (part + 1) * w)
            nc.vector.tensor_tensor(out=wide_sb[h][:, cols], in0=raw_q[h][:, cols].bitcast(FP8), in1=scale_bc[:, cols], op=ALU.mult)

        def turn_x(src, grp_w, slot):
            words = src[:].bitcast(F32)
            for a in range(PASSES // 2):
                tp = tps.tile([P, 2, 2, P], F32, name="tp")
                for g2 in range(2):
                    g = 2 * a + g2
                    for u in range(2):
                        nc.tensor.transpose(out=tp[:, g2, u, :], in_=words[:, 256 * g + u:256 * (g + 1):2], identity=ident[:])
                nc.scalar.copy(out=grp_w[:, 2 * a:2 * a + 2, slot * P:(slot + 1) * P, :], in_=tp[:].rearrange("p g u r -> p g r u"))

        def turn(h, kind):
            if h not in grp_sb:
                grp = grouped.tile([P, 2 * PASSES * P * 4], BF16, name="grp", align_bytes=64)
                grp_sb[h] = grp
            grp_w = grp_sb[h][:].bitcast(F32).rearrange("p (m c u) -> p m c u", m=2 * PASSES, u=2)
            src = wide_sb[h] if kind == 0 else raw_k[h]
            words = src[:].bitcast(F32)
            for a in range(PASSES // 2):
                tp = tps.tile([P, 2, 2, P], F32, name="tp")
                for g2 in range(2):
                    g = 2 * a + g2
                    for u in range(2):
                        nc.tensor.transpose(out=tp[:, u, g2, :], in_=words[:, 256 * g + u:256 * (g + 1):2], identity=ident[:])
                nc.scalar.copy(
                    out=grp_w[:, 4 * a:4 * a + 4, kind * ROT:(kind + 1) * ROT, :],
                    in_=tp[:].rearrange("p u g (x r) -> p (g x) r u", x=2),
                )

        def quantize(h):
            codes = quant.tile([P, 2 * PASSES, P], U32, name="w_codes", align_bytes=64)
            scl = quant.tile([P, 2 * PASSES, P], U8, name="w_scl", align_bytes=64)
            nc.vector.quantize_mx(
                out=codes[:].rearrange("p m c -> p (m c)").bitcast(FP8X4),
                scales=scl[:].rearrange("p m c -> p (m c)"),
                in_=grp_sb[h][:],
            )
            code_sb[h] = (codes, scl)

        def multiply_rot(h):
            codes, scl = code_sb[h]
            acc = accs.tile([P, TOK], F32, name="acc")
            acc_ps[(h, 0)] = acc
            for g in range(PASSES):
                nc.tensor.matmul_mx(
                    out=acc[:],
                    lhsT=codes[:, 2 * g, :].bitcast(FP8X4),
                    lhsT_scale=scl[:, 2 * g, :],
                    rhs=x_codes[:, g, :].bitcast(FP8X4),
                    rhs_scale=x_scl[:, g, :],
                    start=(g == 0),
                    stop=(g == PASSES - 1),
                )

        def add_rot_bias(h):
            by_chan = chan.tile([P, TOK], F32, name="by_chan")
            chan_sb[h] = by_chan
            nc.scalar.activation(out=by_chan[:], in_=acc_ps[(h, 0)][:], func=ACT.Identity, bias=bias_col[:, h:h + 1], scale=1.0)

        def multiply_pass(h, first=0, last=B):
            codes, scl = code_sb[h]
            if first == 0:
                acc = accs.tile([P, TOK], F32, name="acc")
                acc_ps[(h, 1)] = acc
            for b in range(first, last):
                cols = slice(b * P, (b + 1) * P)
                for g in range(PASSES):
                    nc.tensor.matmul_mx(
                        out=acc_ps[(h, 1)][:, cols],
                        lhsT=x_codes[:, g, cols].bitcast(FP8X4),
                        lhsT_scale=x_scl[:, g, cols],
                        rhs=codes[:, 2 * g + 1, :].bitcast(FP8X4),
                        rhs_scale=scl[:, 2 * g + 1, :],
                        start=(g == 0),
                        stop=(g == PASSES - 1),
                    )

        def add_bias(h):
            res = outp.tile([P, B, 2, HD], F32, name="res")
            res_sb[h] = res
            nc.vector.tensor_tensor(
                out=res[:, :, :, ROT:HD],
                in0=acc_ps[(h, 1)][:].rearrange("p (b k r) -> p b k r", b=B, k=2),
                in1=bias_bc[:, h, :, :].unsqueeze(1).to_broadcast([P, B, 2, ROT]),
                op=ALU.add,
            )

        def turn_back(h):
            bt = bts.tile([P, B, HD], F32, name="bt")
            back_sb[h] = bt
            for b in range(B):
                nc.tensor.transpose(out=bt[:, b, :], in_=chan_sb[h][:, b * P:(b + 1) * P], identity=ident[:])

        def cosine_products(h, first, last):
            if first == 0:
                part_c = tmp.tile([P, 2 * B, ROT], F32, name="part_c")
                cos_sb[h] = part_c
            t_v = back_sb[h][:].rearrange("p b (k a f e) -> p (b k a) f e", k=2, a=2, e=2)
            out_v = cos_sb[h][:].rearrange("p n (a f e) -> p (n a) f e", a=2, e=2)
            for f in range(first, last):
                nc.scalar.activation(out=out_v[:, :, f, :], in_=t_v[:, :, f, :], func=ACT.Copy, scale=table[:, 0, 0, 2 * f:2 * f + 1])

        def cosine_on_vector(h):
            part_c = tmp.tile([P, 2 * B, ROT], F32, name="part_c")
            cos_sb[h] = part_c
            nc.vector.tensor_tensor(
                out=part_c[:].rearrange("p (b k) r -> p b (k r)", b=B),
                in0=back_sb[h][:],
                in1=table[:, 0, :, :].rearrange("p k r -> p (k r)").unsqueeze(1).to_broadcast([P, B, 2 * ROT]),
                op=ALU.mult,
            )

        def sine_products(h):
            part_s = tmp.tile([P, 2 * B, ROT], F32, name="part_s")
            sin_sb[h] = part_s
            nc.vector.tensor_tensor(
                out=part_s[:].rearrange("p (b k) (j e) -> p b (k j) e", b=B, e=2),
                in0=back_sb[h][:].rearrange("p b (i e) -> p b i e", e=2)[:, :, :, ::-1],
                in1=table[:, 1, :, :].rearrange("p k (j e) -> p (k j) e", e=2).unsqueeze(1).to_broadcast([P, B, 2 * RD, 2]),
                op=ALU.mult,
            )

        def rotary_add(h, first, last, engine):
            engine.tensor_tensor(
                out=res_sb[h][:, :, first:last, 0:ROT],
                in0=cos_sb[h][:].rearrange("p (b k) r -> p b k r", b=B)[:, :, first:last, :],
                in1=sin_sb[h][:].rearrange("p (b k) r -> p b k r", b=B)[:, :, first:last, :],
                op=ALU.add,
            )

        def add_on_gpsimd(h, after):
            mark = tmp.tile([P, 1], U32, name="mark")
            nc.gpsimd.tensor_copy(out=mark[:], in_=code_sb[after][0][:, 0, 0:1])
            rotary_add(h, 1, 2, nc.gpsimd)

        def store(h):
            nc.sync.dma_start(out=out_0[:, h, :, :].rearrange("b s d -> s b d"), in_=res_sb[h][:, :, 0, :])
            nc.sync.dma_start(out=out_1[:, h, :, :].rearrange("b s d -> s b d"), in_=res_sb[h][:, :, 1, :])

        bias_bc = const.tile([P, NH, 2, ROT], BF16)

        spread_ps = {}

        def spread_bias(half):
            bias_ps = tps.tile([P, 8, P], BF16, name="tp")
            spread_ps[half] = bias_ps
            for i in range(8):
                row = NH + 8 * half + i
                nc.tensor.matmul(out=bias_ps[:, i, :], lhsT=ident_b[:, row:row + 1].to_broadcast([P, P]), rhs=bias_rows[:], start=True, stop=True)

        def copy_bias(half):
            nc.scalar.copy(
                out=bias_bc[:, 8 * half:8 * half + 8, :, :].rearrange("p h k r -> p (h k r)"),
                in_=spread_ps[half][:].rearrange("p h c -> p (h c)"),
            )

        bias_f = const.tile([P, P], F32)
        nc.vector.tensor_copy(out=bias_f[:], in_=bias_rows[:])
        bias_ps = tps.tile([P, 2, 2, P], F32, name="tp")
        nc.tensor.transpose(out=bias_ps[:, 0, 0, :], in_=bias_f[:], identity=ident[:])
        bias_col = const.tile([P, 2 * NH], F32)
        nc.scalar.copy(out=bias_col[:], in_=bias_ps[:, 0, 0, 0:2 * NH])
        for part in range(4):
            widen(0, part, 4)
        xg = const.tile([P, PASSES * TOK * 4], BF16, align_bytes=64)
        xg_w = xg[:].bitcast(F32).rearrange("p (g c u) -> p g c u", g=PASSES, u=2)
        x_codes = const.tile([P, PASSES, TOK], U32, align_bytes=64)
        x_scl = const.tile([P, PASSES, TOK], U8, align_bytes=64)
        turn_x(x_raw[0], xg_w, 0)
        turn_x(x_raw[1], xg_w, 1)
        turn_x(x_raw[2], xg_w, 2)
        turn_x(x_raw[3], xg_w, 3)
        widen(1, 0, 1)
        widen(2, 0, 2)
        for g in range(PASSES):
            nc.vector.quantize_mx(
                out=x_codes[:, g, :].bitcast(FP8X4),
                scales=x_scl[:, g, :],
                in_=xg[:, g * TOK * 4:(g + 1) * TOK * 4],
            )
        turn(0, 0)
        turn(0, 1)
        quantize(0)
        widen(2, 1, 2)
        turn(1, 1)
        turn(1, 0)
        spread_bias(0)
        quantize(1)
        nc.scalar.activation(
            out=table[:],
            in_=red[:].rearrange("p (c r) -> p c r", c=2).unsqueeze(2).to_broadcast([P, 2, 2, ROT]),
            func=ACT.Sin,
        )

        for j in range(NH):
            if j + AHEAD < NH:
                load_q(j + AHEAD)
                load_k(j + AHEAD)
            if j == 0:
                multiply_rot(0)
            if j + 2 < NH:
                turn(j + 2, 1)
            if j >= 1:
                add_bias(j - 1)
                turn_back(j - 1)
                if j < NH - 1:
                    cosine_products(j - 1, 0, 8)
            if j >= 2:
                sine_products(j - 2)
            if 3 <= j < NH - 1:
                add_on_gpsimd(j - 3, j + 1)
                store(j - 3)
            if j >= 1:
                multiply_rot(j)
            add_rot_bias(j)
            if j + 3 < NH:
                widen(j + 3, 0, 1)
            if j >= 2:
                rotary_add(j - 2, 0, 1, nc.vector)
            if j + 2 < NH:
                turn(j + 2, 0)
                quantize(j + 2)
            if 1 <= j < NH - 1:
                cosine_products(j - 1, 8, RD // 2)
            if j == 0:
                copy_bias(0)
            if j == 4:
                spread_bias(1)
                copy_bias(1)
            if j < NH - 1:
                multiply_pass(j)

        last = NH - 1
        multiply_pass(last, 0, 2)
        turn_back(last)
        rotary_add(last - 3, 1, 2, nc.gpsimd)
        store(last - 3)
        rotary_add(last - 2, 1, 2, nc.gpsimd)
        store(last - 2)
        cosine_on_vector(last - 1)
        sine_products(last - 1)
        rotary_add(last - 1, 0, 2, nc.vector)
        store(last - 1)
        cosine_on_vector(last)
        sine_products(last)
        multiply_pass(last, 2, 4)
        add_bias(last)
        rotary_add(last, 0, 2, nc.vector)
        store(last)
